import numpy as np
import ml_dtypes


def mxq(x, axis, fmt="e4m3"):
    dtype, down = {"e4m3": (ml_dtypes.float8_e4m3fn, 7), "e5m2": (ml_dtypes.float8_e5m2, 14)}[fmt]
    v = np.moveaxis(np.asarray(x, np.float32).astype(ml_dtypes.bfloat16).astype(np.float64), axis, -1)
    blocks = v.reshape(v.shape[:-1] + (-1, 32))
    amax = np.abs(blocks).max(-1, keepdims=True)
    byte = np.maximum(np.where(amax > 0, np.frexp(amax)[1] - 1 + 127, 0) - down, 1)
    scale = np.exp2(byte - 127.0)
    codes = (blocks / scale).astype(np.float32).astype(dtype).astype(np.float64)
    return np.moveaxis((codes * scale).reshape(v.shape), -1, axis)


WIDE = False


def mx_kscale(k):
    if not WIDE:
        return np.ones(k)
    levels = np.array([10, -10, 5, -5, 0])
    if k % 512:
        return np.exp2(np.random.permutation(np.resize(levels, k // 32))).repeat(32)
    a = np.empty((k // 512, 16))
    for p in range(k // 512):
        a[p, :8] = np.random.permutation(np.resize(levels, 8))
        for g in range(8):
            far = levels[np.abs(levels - a[p, g]) >= 10]
            a[p, g + 8] = far[np.random.randint(len(far))]
    return np.exp2(a.ravel()).repeat(32)


BF16 = ml_dtypes.bfloat16


def bf(x):
    return np.asarray(x, np.float32).astype(BF16)


def f64(x):
    return np.asarray(x).astype(np.float64)


B, C, H, W, K, HID, LAT = 4, 512, 16, 16, 8, 512, 32
REDUCTION = -0.1
CLAMP = 500.0
HOT = 1.2 * CLAMP / (-REDUCTION * C * np.sqrt(2.0 / np.pi))


def setup_inputs():
    s = mx_kscale(HID)
    amp = np.where(np.random.random((B, 1, H, W)) < 0.125, HOT, 1.0)
    return {"d": bf(np.tanh(np.random.standard_normal((K, B, HID, H, W))) * s[:, None, None]),
            "W_dec": bf(np.random.standard_normal((K, C, HID)) * 1.1 / np.sqrt(HID) / s),
            "x": bf(np.random.standard_normal((B, C, H, W)) * amp)}


def reference(d, W_dec, x):
    xf = f64(x)
    wq = mxq(f64(W_dec), 2, "e4m3")
    dq = mxq(f64(d), 2, "e4m3")
    recon = (wq[:, None] @ dq.reshape(K, B, HID, H * W)).reshape(K, B, C, H, W)
    err = np.sum(np.abs(recon - xf[None]), axis=2) * REDUCTION
    logits = np.swapaxes(np.clip(err, -CLAMP, CLAMP), 0, 1)
    e = np.exp(logits - logits.max(axis=1, keepdims=True))
    p = e / e.sum(axis=1, keepdims=True)
    error = np.mean(logits, axis=(2, 3))
    return p, error, np.swapaxes(recon, 0, 1)

@@ -1,0 +1,372 @@
+from contextlib import ExitStack
+
+import concourse.mybir as mybir
+from concourse.masks import make_identity
+
+FP8X4 = mybir.dt.float8_e4m3fn_x4
+BF16 = mybir.dt.bfloat16
+F32 = mybir.dt.float32
+U32 = mybir.dt.uint32
+U8 = mybir.dt.uint8
+ALU = mybir.AluOpType
+ACT = mybir.ActivationFunctionType
+AX = mybir.AxisListType
+
+P = 128
+NK, NB, NC, NJ, NW = 8, 4, 512, 512, 256
+FLOPS = 2 * NK * NB * NC * NJ * NW
+
+MANUAL = False
+
+
+def tile_cssrclassifier_pa_kernel(tc, d, W_dec, x, out_0, out_1, out_2):
+    nc = tc.nc
+    with ExitStack() as ctx:
+        const = ctx.enter_context(tc.tile_pool(name="const", bufs=1))
+        raw = ctx.enter_context(tc.tile_pool(name="raw", bufs=NK))
+        grp = ctx.enter_context(tc.tile_pool(name="grp", bufs=3))
+        mx = ctx.enter_context(tc.tile_pool(name="mx", bufs=3))
+        recp = ctx.enter_context(tc.tile_pool(name="recp", bufs=6))
+        junk = ctx.enter_context(tc.tile_pool(name="junk", bufs=2))
+        aux = ctx.enter_context(tc.psum_pool(name="aux", bufs=8))
+        ps_a = aux
+        ps_b = aux
+        if MANUAL:
+            ctx.enter_context(tc.manual_schedule())
+
+        warm = const.tile([P, 1], F32)
+        nc.vector.memset(warm[:], 0.0)
+        warm2 = const.tile([P, 1], F32)
+        nc.scalar.activation(out=warm2[:], in_=warm[:], func=ACT.Exp)
+        ident_f = const.tile([P, P], F32)
+        make_identity(nc, ident_f[:])
+        ident_b = const.tile([P, P], BF16)
+        make_identity(nc, ident_b[:])
+        ones_f = const.tile([P, P], F32)
+        nc.vector.memset(ones_f[:], 1.0 / NW)
+        pad = const.tile([P, P], F32)
+        nc.vector.memset(pad[:], 0.0)
+
+        smax = const.tile([P, 64], F32)
+        sr01 = const.tile([P, 64], F32)
+        sx = const.tile([P, 8], F32)
+        sx01 = const.tile([P, 8], F32)
+        x_sb = const.tile([P, NB, 4, NW], BF16)
+        x_t = const.tile([P, 8, NC], BF16)
+
+        state = {}
+
+        def load_w(k):
+            wr = raw.tile([P, 4, NJ], BF16, name="w_raw%d" % k, tag="w_raw")
+            nc.sync.dma_start(out=wr[:], in_=W_dec[k].rearrange("(p t) j -> p t j", t=4))
+            state[("w_raw", k)] = wr
+
+        def load_d(k, bp):
+            if bp == 0:
+                dr_new = raw.tile([P, NB, 4, NW], BF16, name="d_raw%d" % k, tag="d_raw")
+                state[("d_raw", k)] = dr_new
+            dr = state[("d_raw", k)]
+            nc.sync.dma_start(
+                out=dr[:, 2 * bp : 2 * bp + 2].rearrange("q b t w -> q b (t w)"),
+                in_=d[k, 2 * bp : 2 * bp + 2].rearrange("b (q t) h w -> q b (t h w)", t=4),
+            )
+
+        def load_x(bp):
+            nc.sync.dma_start(
+                out=x_sb[:, 2 * bp : 2 * bp + 2].rearrange("p b t w -> p b (t w)"),
+                in_=x[2 * bp : 2 * bp + 2].rearrange("b (p t) h w -> p b (t h w)", t=4),
+            )
+
+        load_w(0)
+        load_d(0, 0)
+        load_x(0)
+        load_d(0, 1)
+        load_x(1)
+        for k in range(1, NK):
+            load_w(k)
+            load_d(k, 0)
+            load_d(k, 1)
+
+        def w_t(k):
+            wf = state[("w_raw", k)][:].bitcast(F32)
+            for g in range(2):
+                wt = aux.tile([P, 4, P], F32, name="wt%d_%d" % (k, g), tag="aux")
+                for tt in range(2):
+                    for u in range(2):
+                        nc.tensor.transpose(wt[:, tt * 2 + u, :], wf[:, 2 * g + tt, u : 2 * P : 2], ident_f[:])
+                state[("wt", k, g)] = wt
+
+        def w_exit(k, g):
+            if g == 0:
+                wg_new = grp.tile([P, NC, 4], BF16, name="wg%d" % k, tag="wg", align_bytes=64)
+                state[("wg", k)] = wg_new
+            wgf = state[("wg", k)][:].bitcast(F32)
+            nc.scalar.copy(
+                out=wgf[:, g * 256 : (g + 1) * 256, :].rearrange("q (tt p) u -> q tt p u", tt=2),
+                in_=state[("wt", k, g)][:].rearrange("q (tt u) p -> q tt p u", u=2),
+            )
+
+        def q_w(k):
+            wg = state[("wg", k)]
+            wc = mx.tile([P, NC], U32, name="wc%d" % k, tag="wc", align_bytes=64)
+            ws = mx.tile([P, NC], U8, name="ws%d" % k, tag="ws", align_bytes=64)
+            nc.vector.quantize_mx(out=wc[:].bitcast(FP8X4), scales=ws[:], in_=wg[:].rearrange("q c t -> q (c t)"))
+            state[("wc", k)] = wc
+            state[("ws", k)] = ws
+
+        def d_views(k):
+            if ("dg", k) not in state:
+                dg_new = grp.tile([P, NB, NW, 4], BF16, name="dg%d" % k, tag="dg", align_bytes=64)
+                state[("dg", k)] = dg_new
+            src = state[("d_raw", k)][:].rearrange("q b t (c i) -> q b c t i", i=4)
+            dst = state[("dg", k)][:].rearrange("q b (c i) t -> q b c t i", i=4)
+            return src, dst
+
+        def rg_v(k, b0, b1):
+            src, dst = d_views(k)
+            if b1 - b0 == 1:
+                nc.vector.tensor_copy(out=dst[:, b0], in_=src[:, b0])
+            else:
+                nc.vector.tensor_copy(out=dst[:, b0:b1], in_=src[:, b0:b1])
+
+        def rg_s(k, b, half):
+            src, dst = d_views(k)
+            cs = slice(half * 32, (half + 1) * 32)
+            nc.scalar.copy(out=dst[:, b, cs], in_=src[:, b, cs])
+
+        def q_d(k, bp):
+            if ("dc", k) not in state:
+                dc_new = mx.tile([P, NB * NW], U32, name="dc%d" % k, tag="dc", align_bytes=64)
+                ds_new = mx.tile([P, NB * NW], U8, name="ds%d" % k, tag="ds", align_bytes=64)
+                state[("dc", k)] = dc_new
+                state[("ds", k)] = ds_new
+            cols = slice(bp * 512, (bp + 1) * 512)
+            nc.vector.quantize_mx(
+                out=state[("dc", k)][:, cols].bitcast(FP8X4),
+                scales=state[("ds", k)][:, cols],
+                in_=state[("dg", k)][:, 2 * bp : 2 * bp + 2].rearrange("q b w t -> q (b w t)"),
+            )
+
+        def x_tr(b):
+            xp = aux.tile([P, 2, NC], BF16, name="xp%d" % b, tag="aux")
+            for h in range(2):
+                for t in range(4):
+                    nc.tensor.transpose(xp[:, h, t * P : (t + 1) * P], x_sb[:, b, t, h * P : (h + 1) * P], ident_b[:])
+            state[("xp", b)] = xp
+
+        def x_exit(b):
+            xp = state[("xp", b)]
+            for h in range(2):
+                i = 2 * b + h
+                nc.scalar.activation(out=x_t[:, i, :], in_=xp[:, h, :], func=ACT.Copy, accum_out=sx[:, i : i + 1])
+
+        def ops(k):
+            return state[("wc", k)], state[("ws", k)], state[("dc", k)], state[("ds", k)]
+
+        def mm_a(k, i):
+            bp, t = divmod(i, 4)
+            wc, ws, dc, ds = ops(k)
+            pa = ps_a.tile([P, 512], F32, name="pa%d_%d" % (k, i), tag="aux")
+            mc = slice(t * P, (t + 1) * P)
+            ncol = slice(bp * 512, (bp + 1) * 512)
+            nc.tensor.matmul_mx(
+                out=pa[:],
+                lhsT=wc[:, mc].bitcast(FP8X4),
+                lhsT_scale=ws[:, mc],
+                rhs=dc[:, ncol].bitcast(FP8X4),
+                rhs_scale=ds[:, ncol],
+                start=True,
+                stop=True,
+            )
+            state[("pa", k, i)] = pa
+
+        def copy_a(k, i, eng):
+            bp, t = divmod(i, 4)
+            if t == 0:
+                rec_new = recp.tile([P, 2, 4, NW], F32, name="rec%d_%d" % (k, bp), tag="rec")
+                state["rec"] = rec_new
+            rec = state["rec"]
+            nc.scalar.copy(out=rec[:, :, t, :], in_=state[("pa", k, i)][:].rearrange("p (b w) -> p b w", b=2))
+            if t == 3:
+                eng.dma_start(
+                    out=out_2[2 * bp : 2 * bp + 2, k].rearrange("b (p t) h w -> p b (t h w)", t=4),
+                    in_=rec[:].rearrange("p b t w -> p b (t w)"),
+                )
+
+        def mm_b(k, i):
+            wc, ws, dc, ds = ops(k)
+            mc = slice(i * P, (i + 1) * P)
+            pb = ps_b.tile([P, 512], F32, name="pb%d_%d" % (k, i), tag="aux")
+            nc.tensor.matmul_mx(
+                out=pb[:],
+                lhsT=dc[:, mc].bitcast(FP8X4),
+                lhsT_scale=ds[:, mc],
+                rhs=wc[:].bitcast(FP8X4),
+                rhs_scale=ws[:],
+                start=True,
+                stop=True,
+            )
+            state[("pb", k, i)] = pb
+            g = i % 4
+            if g == 0:
+                pc_new = aux.tile([P, 4, P], F32, name="pc%d_%d" % (k, i), tag="aux")
+                state[("pc", k, i // 4)] = pc_new
+            pc = state[("pc", k, i // 4)]
+            for t in range(4):
+                tcol = slice(t * P, (t + 1) * P)
+                nc.tensor.matmul_mx(
+                    out=pc[:, g, :],
+                    lhsT=dc[:, mc].bitcast(FP8X4),
+                    lhsT_scale=ds[:, mc],
+                    rhs=wc[:, tcol].bitcast(FP8X4),
+                    rhs_scale=ws[:, tcol],
+                    start=(t == 0),
+                    stop=(t == 3),
+                )
+
+        def col_of(k, i):
+            return (i // 2) * 16 + k * 2 + (i % 2)
+
+        def stt(k, i):
+            col = col_of(k, i)
+            jk = junk.tile([P, 512], BF16, name="jk%d_%d" % (k, i), tag="jk")
+            nc.vector.scalar_tensor_tensor(
+                out=jk[:],
+                in0=state[("pb", k, i)][:],
+                scalar=1.0,
+                in1=x_t[:, i, :],
+                op0=ALU.mult,
+                op1=ALU.max,
+                accum_out=smax[:, col : col + 1],
+            )
+
+        def cacc(k, grp_i):
+            pc = state[("pc", k, grp_i)]
+            for gg in range(4):
+                col = col_of(k, grp_i * 4 + gg)
+                jc = junk.tile([P, P], BF16, name="jc%d_%d_%d" % (k, grp_i, gg), tag="jc")
+                nc.scalar.activation(
+                    out=jc[:], in_=pc[:, gg, :], func=ACT.Copy, scale=0.1, accum_out=sr01[:, col : col + 1]
+                )
+
+        w_t(0)
+        w_exit(0, 0)
+        w_exit(0, 1)
+        x_tr(0)
+        x_tr(1)
+        x_exit(0)
+        x_exit(1)
+        rg_v(0, 0, 1)
+        rg_v(0, 1, 2)
+        q_w(0)
+        q_d(0, 0)
+
+        for k in range(NK - 1):
+            for i in range(8):
+                mm_b(k, i)
+                mm_a(k, i)
+                stt(k, i)
+                copy_a(k, i, nc.gpsimd)
+                if k == 0:
+                    if i == 0:
+                        x_tr(2)
+                        x_tr(3)
+                        x_exit(2)
+                        rg_v(0, 2, 4)
+                    elif i == 1:
+                        x_exit(3)
+                    elif i == 2:
+                        q_d(0, 1)
+                    elif i == 3:
+                        nc.vector.tensor_scalar_mul(out=sx01[:], in0=sx[:], scalar1=0.1)
+                else:
+                    if i == 0:
+                        cacc(k - 1, 1)
+                    elif i == 1:
+                        q_d(k, 1)
+                if i == 1:
+                    w_t(k + 1)
+                elif i == 2:
+                    w_exit(k + 1, 0)
+                elif i == 3:
+                    w_exit(k + 1, 1)
+                    rg_v(k + 1, 0, 1)
+                elif i == 4:
+                    cacc(k, 0)
+                    rg_v(k + 1, 1, 2)
+                elif i == 5:
+                    rg_s(k + 1, 3, 0)
+                    q_w(k + 1)
+                elif i == 6:
+                    rg_s(k + 1, 3, 1)
+                    q_d(k + 1, 0)
+                elif i == 7:
+                    rg_v(k + 1, 2, 3)
+
+        k = NK - 1
+        for g in range(4):
+            mm_b(k, 2 * g)
+            mm_b(k, 2 * g + 1)
+            mm_a(k, g)
+            stt(k, 2 * g)
+            stt(k, 2 * g + 1)
+            copy_a(k, g, nc.sync)
+            if g == 0:
+                cacc(k - 1, 1)
+                q_d(k, 1)
+            elif g == 2:
+                cacc(k, 0)
+        cacc(k, 1)
+        for i in range(4, 8):
+            mm_a(k, i)
+            copy_a(k, i, nc.scalar)
+
+        def v4(ap):
+            return ap.rearrange("p (b k h) -> p b k h", b=NB, k=NK, h=2)
+
+        def bc(ap):
+            return ap.rearrange("p (b h) -> p b h", h=2).unsqueeze(2).to_broadcast([P, NB, NK, 2])
+
+        def by_group(ap):
+            return ap.rearrange("p (b k h) -> p b h k", b=NB, k=NK, h=2)
+
+        def groups(ap):
+            return ap.rearrange("p (b h) -> p b h", h=2)
+
+        srx = const.tile([P, 64], F32)
+        nc.vector.tensor_tensor(out=v4(srx[:]), in0=v4(sr01[:]), in1=bc(sx01[:]), op=ALU.add)
+        t1 = const.tile([P, 64], F32)
+        nc.vector.scalar_tensor_tensor(out=t1[:], in0=smax[:], scalar=-0.2, in1=srx[:], op0=ALU.mult, op1=ALU.add)
+        lg = const.tile([P, 64], F32)
+        nc.vector.tensor_scalar(out=lg[:], in0=t1[:], scalar1=-500.0, scalar2=500.0, op0=ALU.max, op1=ALU.min)
+        mxk = const.tile([P, 8], F32)
+        nc.vector.tensor_reduce(out=groups(mxk[:]), in_=by_group(lg[:]), axis=AX.X, op=ALU.max)
+        sh = const.tile([P, 64], F32)
+        nc.vector.tensor_tensor(out=v4(sh[:]), in0=v4(lg[:]), in1=bc(mxk[:]), op=ALU.subtract)
+        ex = const.tile([P, 64], F32)
+        nc.scalar.activation(out=ex[:], in_=sh[:], func=ACT.Exp)
+        den = const.tile([P, 8], F32)
+        nc.vector.tensor_reduce(out=groups(den[:]), in_=by_group(ex[:]), axis=AX.X, op=ALU.add)
+        rden = const.tile([P, 8], F32)
+        nc.vector.reciprocal(out=rden[:], in_=den[:])
+        nc.vector.tensor_tensor(out=v4(pad[:, 0:64]), in0=v4(ex[:]), in1=bc(rden[:]), op=ALU.mult)
+        pt = aux.tile([P, P], F32, name="pt", tag="aux")
+        nc.tensor.transpose(pt[:], pad[:], ident_f[:])
+        lsum = const.tile([P, 32], F32)
+        lg3 = lg[:].rearrange("p (c h) -> p c h", h=2)
+        nc.vector.tensor_tensor(out=lsum[:], in0=lg3[:, :, 0], in1=lg3[:, :, 1], op=ALU.add)
+        pmean = aux.tile([P, 32], F32, name="pmean", tag="aux")
+        nc.tensor.matmul(out=pmean[:], lhsT=ones_f[:], rhs=lsum[:], start=True, stop=True)
+        p_out = const.tile([P, P], F32)
+        nc.vector.tensor_copy(out=p_out[:], in_=pt[:])
+        nc.sync.dma_start(out=out_0.rearrange("b k (h r) w -> (b k h) (r w)", h=2), in_=p_out[0:64, :])
+        e_sel = const.tile([P, NB, NK], F32)
+        nc.vector.tensor_tensor(
+            out=e_sel[:],
+            in0=pmean[:].rearrange("p (b k) -> p b k", b=NB),
+            in1=ident_f[:, 0:NB].unsqueeze(2).to_broadcast([P, NB, NK]),
+            op=ALU.mult,
+        )
+        e_out = const.tile([P, NK], F32)
+        nc.vector.tensor_reduce(out=e_out[:], in_=e_sel[:].rearrange("p b k -> p k b"), axis=AX.X, op=ALU.add)
+        nc.sync.dma_start(out=out_1, in_=e_out[0:NB, :])

@@ -16,7 +16,22 @@ P = 128
 NK, NB, NC, NJ, NW = 8, 4, 512, 512, 256
 FLOPS = 2 * NK * NB * NC * NJ * NW
 
-MANUAL = False
+GRP = 2
+AHEAD = 4
+MANUAL = True
+PA, PB, PCB, WT = 2, 2, 2, 2
+PE_FIRST = "T0 T1 X0 b0 b1 X1 c0 b2 c1 a0 a1 X2 X3 b3 c2 a2 T0+ T1+ b4 c3 a3 b5 c4 a4 b6 c5 a5 b7 c6 a6 b0+ c7 a7"
+PE_STEADY = "b1 c0 a0 b2 c1 a1 T0+ T1+ b3 c2 a2 b4 c3 a3 b5 c4 a4 b6 c5 a5 b7 c6 a6 b0+ c7 a7"
+V_FIRST = "r0 W d0 r1 s0 d1 s1 r2 s2 r3 s3 D1 r0+ s4 r1+ s5 W+ s6 D0+ s7 r2+"
+V_STEADY = "s0 D1 s1 r0+ s2 r1+ s3 r2+ s4 s5 W+ s6 D0+ s7"
+S_FIRST = "e0 e1 x0 x1 C0 A0 x2 C1 A1 x3 C2 A2 e0+ e1+ C3 A3 C4 A4 C5 A5 C6 A6 C7 r3a+ A7 r3b+"
+S_STEADY = "C0 A0 C1 A1 e0+ C2 A2 e1+ C3 A3 C4 A4 r3a+ C5 A5 r3b+ C6 A6 C7 A7"
+PE_LAST = "b1 c0 a0 Y0 Y1 Y2 Y3 b2 c1 a1 b3 c2 a2 b4 c3 a3 b5 c4 b6 c5 b7 c6 c7 a4 a5 a6 a7"
+V_LAST = "s0 D1 s1 xs s2 s3 s4 s5 s6 s7"
+S_LAST = "C0 A0 C1 A1 C2 A2 C3 A3 C4 C5 C6 C7 A4 A5 A6 A7"
+G_LAST = ""
+G_FIRST = ""
+G_STEADY = ""
 
 
 def tile_cssrclassifier_pa_kernel(tc, d, W_dec, x, out_0, out_1, out_2):
@@ -24,87 +39,97 @@ def tile_cssrclassifier_pa_kernel(tc, d, W_dec, x, out_0, out_1, out_2):
     with ExitStack() as ctx:
         const = ctx.enter_context(tc.tile_pool(name="const", bufs=1))
         raw = ctx.enter_context(tc.tile_pool(name="raw", bufs=NK))
-        grp = ctx.enter_context(tc.tile_pool(name="grp", bufs=3))
+        grp = ctx.enter_context(tc.tile_pool(name="grp", bufs=GRP))
         mx = ctx.enter_context(tc.tile_pool(name="mx", bufs=3))
         recp = ctx.enter_context(tc.tile_pool(name="recp", bufs=6))
         junk = ctx.enter_context(tc.tile_pool(name="junk", bufs=2))
-        aux = ctx.enter_context(tc.psum_pool(name="aux", bufs=8))
-        ps_a = aux
-        ps_b = aux
+        ps_a = ctx.enter_context(tc.psum_pool(name="ps_a", bufs=PA))
+        ps_b = ctx.enter_context(tc.psum_pool(name="ps_b", bufs=PB))
+        ps_c = ctx.enter_context(tc.psum_pool(name="ps_c", bufs=PCB))
+        ps_t = ctx.enter_context(tc.psum_pool(name="ps_t", bufs=WT))
         if MANUAL:
             ctx.enter_context(tc.manual_schedule())
 
-        warm = const.tile([P, 1], F32)
-        nc.vector.memset(warm[:], 0.0)
-        warm2 = const.tile([P, 1], F32)
-        nc.scalar.activation(out=warm2[:], in_=warm[:], func=ACT.Exp)
+        smax = const.tile([P, 64], F32)
+        sr01 = const.tile([P, 64], F32)
+        sx01 = const.tile([P, 8], F32)
+        x_sb = const.tile([P, NB, 4, NW], BF16)
+        x_t = const.tile([P, 8, NC], BF16)
+        state = {}
+
+        def load_w(k, t0=0, t1=4):
+            if t0 == 0:
+                wr = raw.tile([P, 4, NJ], BF16, name="w_raw%d" % k, tag="w_raw")
+                state[("w_raw", k)] = wr
+            wr = state[("w_raw", k)]
+            nc.sync.dma_start(out=wr[:, t0:t1], in_=W_dec[k].rearrange("(p t) j -> p t j", t=4)[:, t0:t1])
+
+        def load_d(k, b0, b1):
+            if b0 == 0:
+                dr_new = raw.tile([P, NB, 4, NW], BF16, name="d_raw%d" % k, tag="d_raw")
+                state[("d_raw", k)] = dr_new
+            dr = state[("d_raw", k)]
+            nc.sync.dma_start(
+                out=dr[:, b0:b1].rearrange("q b t w -> q b (t w)"),
+                in_=d[k, b0:b1].rearrange("b (q t) h w -> q b (t h w)", t=4),
+            )
+
+        def load_x(b0, b1):
+            nc.sync.dma_start(
+                out=x_sb[:, b0:b1].rearrange("p b t w -> p b (t w)"),
+                in_=x[b0:b1].rearrange("b (p t) h w -> p b (t h w)", t=4),
+            )
+
+        load_w(0, 0, 2)
+        load_w(0, 2, 4)
+        load_d(0, 0, 1)
+        load_x(0, 1)
+        load_d(0, 1, 2)
+        load_x(1, 2)
+        load_d(0, 2, 4)
+        load_x(2, 4)
+        def load_class(k):
+            load_w(k)
+            load_d(k, 0, 2)
+            load_d(k, 2, 4)
+
+        for k in range(1, AHEAD):
+            load_class(k)
+
         ident_f = const.tile([P, P], F32)
         make_identity(nc, ident_f[:])
         ident_b = const.tile([P, P], BF16)
         make_identity(nc, ident_b[:])
+        ones_b = const.tile([P, 1], BF16)
+        nc.vector.memset(ones_b[:], 1.0)
+        warm = const.tile([P, 1], F32)
+        nc.vector.memset(warm[:], 0.0)
+        warm2 = const.tile([P, 1], F32)
+        nc.scalar.activation(out=warm2[:], in_=warm[:], func=ACT.Exp)
         ones_f = const.tile([P, P], F32)
         nc.vector.memset(ones_f[:], 1.0 / NW)
         pad = const.tile([P, P], F32)
         nc.vector.memset(pad[:], 0.0)
 
-        smax = const.tile([P, 64], F32)
-        sr01 = const.tile([P, 64], F32)
-        sx = const.tile([P, 8], F32)
-        sx01 = const.tile([P, 8], F32)
-        x_sb = const.tile([P, NB, 4, NW], BF16)
-        x_t = const.tile([P, 8, NC], BF16)
-
-        state = {}
-
-        def load_w(k):
-            wr = raw.tile([P, 4, NJ], BF16, name="w_raw%d" % k, tag="w_raw")
-            nc.sync.dma_start(out=wr[:], in_=W_dec[k].rearrange("(p t) j -> p t j", t=4))
-            state[("w_raw", k)] = wr
-
-        def load_d(k, bp):
-            if bp == 0:
-                dr_new = raw.tile([P, NB, 4, NW], BF16, name="d_raw%d" % k, tag="d_raw")
-                state[("d_raw", k)] = dr_new
-            dr = state[("d_raw", k)]
-            nc.sync.dma_start(
-                out=dr[:, 2 * bp : 2 * bp + 2].rearrange("q b t w -> q b (t w)"),
-                in_=d[k, 2 * bp : 2 * bp + 2].rearrange("b (q t) h w -> q b (t h w)", t=4),
-            )
-
-        def load_x(bp):
-            nc.sync.dma_start(
-                out=x_sb[:, 2 * bp : 2 * bp + 2].rearrange("p b t w -> p b (t w)"),
-                in_=x[2 * bp : 2 * bp + 2].rearrange("b (p t) h w -> p b (t h w)", t=4),
-            )
-
-        load_w(0)
-        load_d(0, 0)
-        load_x(0)
-        load_d(0, 1)
-        load_x(1)
-        for k in range(1, NK):
-            load_w(k)
-            load_d(k, 0)
-            load_d(k, 1)
-
-        def w_t(k):
+        def w_t(k, g):
             wf = state[("w_raw", k)][:].bitcast(F32)
-            for g in range(2):
-                wt = aux.tile([P, 4, P], F32, name="wt%d_%d" % (k, g), tag="aux")
-                for tt in range(2):
-                    for u in range(2):
-                        nc.tensor.transpose(wt[:, tt * 2 + u, :], wf[:, 2 * g + tt, u : 2 * P : 2], ident_f[:])
-                state[("wt", k, g)] = wt
+            wt = ps_t.tile([P, 4, P], F32, name="wt%d_%d" % (k, g), tag="tr")
+            for tt in range(2):
+                for u in range(2):
+                    nc.tensor.transpose(wt[:, tt * 2 + u, :], wf[:, 2 * g + tt, u : 2 * P : 2], ident_f[:])
+            state[("wt", k, g)] = wt
 
-        def w_exit(k, g):
+        def w_exit(k, g, eng="s"):
             if g == 0:
                 wg_new = grp.tile([P, NC, 4], BF16, name="wg%d" % k, tag="wg", align_bytes=64)
                 state[("wg", k)] = wg_new
             wgf = state[("wg", k)][:].bitcast(F32)
-            nc.scalar.copy(
-                out=wgf[:, g * 256 : (g + 1) * 256, :].rearrange("q (tt p) u -> q tt p u", tt=2),
-                in_=state[("wt", k, g)][:].rearrange("q (tt u) p -> q tt p u", u=2),
-            )
+            o = wgf[:, g * 256 : (g + 1) * 256, :].rearrange("q (tt p) u -> q tt p u", tt=2)
+            i = state[("wt", k, g)][:].rearrange("q (tt u) p -> q tt p u", u=2)
+            if eng == "s":
+                nc.scalar.copy(out=o, in_=i)
+            else:
+                nc.vector.tensor_copy(out=o, in_=i)
 
         def q_w(k):
             wg = state[("wg", k)]
@@ -114,51 +139,79 @@ def tile_cssrclassifier_pa_kernel(tc, d, W_dec, x, out_0, out_1, out_2):
             state[("wc", k)] = wc
             state[("ws", k)] = ws
 
-        def d_views(k):
-            if ("dg", k) not in state:
-                dg_new = grp.tile([P, NB, NW, 4], BF16, name="dg%d" % k, tag="dg", align_bytes=64)
-                state[("dg", k)] = dg_new
-            src = state[("d_raw", k)][:].rearrange("q b t (c i) -> q b c t i", i=4)
-            dst = state[("dg", k)][:].rearrange("q b (c i) t -> q b c t i", i=4)
-            return src, dst
+        def dg_of(k, b):
+            key = ("dg", k, b // 2)
+            if key not in state:
+                dg_new = grp.tile([P, 2, NW, 4], BF16, name="dg%d_%d" % (k, b // 2), tag="dg%d" % (b // 2), align_bytes=64)
+                state[key] = dg_new
+            return state[key]
 
-        def rg_v(k, b0, b1):
-            src, dst = d_views(k)
-            if b1 - b0 == 1:
-                nc.vector.tensor_copy(out=dst[:, b0], in_=src[:, b0])
+        def rg(k, b, h0, h1, eng):
+            if eng == "G":
+                ws = slice(h0 * NW // 2, h1 * NW // 2)
+                nc.gpsimd.tensor_scalar(
+                    out=dg_of(k, b)[:, b % 2, ws],
+                    in0=state[("d_raw", k)][:, b, :, ws].rearrange("q t w -> q w t"),
+                    scalar1=1.0,
+                    scalar2=0.0,
+                    op0=ALU.mult,
+                    op1=ALU.add,
+                )
+                return
+            cs = slice(h0 * 32, h1 * 32)
+            src = state[("d_raw", k)][:, b].rearrange("q t (c i) -> q c t i", i=4)[:, cs]
+            dst = dg_of(k, b)[:, b % 2].rearrange("q (c i) t -> q c t i", i=4)[:, cs]
+            if eng == "V":
+                nc.vector.tensor_copy(out=dst, in_=src)
             else:
-                nc.vector.tensor_copy(out=dst[:, b0:b1], in_=src[:, b0:b1])
+                nc.scalar.copy(out=dst, in_=src)
 
-        def rg_s(k, b, half):
-            src, dst = d_views(k)
-            cs = slice(half * 32, (half + 1) * 32)
-            nc.scalar.copy(out=dst[:, b, cs], in_=src[:, b, cs])
-
-        def q_d(k, bp):
+        def q_d_cols(k, b0, b1):
             if ("dc", k) not in state:
                 dc_new = mx.tile([P, NB * NW], U32, name="dc%d" % k, tag="dc", align_bytes=64)
                 ds_new = mx.tile([P, NB * NW], U8, name="ds%d" % k, tag="ds", align_bytes=64)
                 state[("dc", k)] = dc_new
                 state[("ds", k)] = ds_new
-            cols = slice(bp * 512, (bp + 1) * 512)
+            cols = slice(b0 * NW, b1 * NW)
             nc.vector.quantize_mx(
                 out=state[("dc", k)][:, cols].bitcast(FP8X4),
                 scales=state[("ds", k)][:, cols],
-                in_=state[("dg", k)][:, 2 * bp : 2 * bp + 2].rearrange("q b w t -> q (b w t)"),
+                in_=dg_of(k, b0)[:, b0 % 2 : b0 % 2 + b1 - b0].rearrange("q b w t -> q (b w t)"),
             )
 
+        def q_d(k, bp):
+            q_d_cols(k, 2 * bp, 2 * bp + 2)
+
         def x_tr(b):
-            xp = aux.tile([P, 2, NC], BF16, name="xp%d" % b, tag="aux")
+            xp = ps_t.tile([P, 2, NC], BF16, name="xp%d" % b, tag="tr")
             for h in range(2):
                 for t in range(4):
                     nc.tensor.transpose(xp[:, h, t * P : (t + 1) * P], x_sb[:, b, t, h * P : (h + 1) * P], ident_b[:])
             state[("xp", b)] = xp
 
-        def x_exit(b):
+        def x_exit(b, eng="s"):
             xp = state[("xp", b)]
+            o = x_t[:, 2 * b : 2 * b + 2, :]
+            if eng == "s":
+                nc.scalar.copy(out=o, in_=xp[:])
+            else:
+                nc.vector.tensor_copy(out=o, in_=xp[:])
+
+        def x_sum(b):
+            if b == 0:
+                state["sxp"] = ps_t.tile([P, 8], F32, name="sxp", tag="tr")
             for h in range(2):
-                i = 2 * b + h
-                nc.scalar.activation(out=x_t[:, i, :], in_=xp[:, h, :], func=ACT.Copy, accum_out=sx[:, i : i + 1])
+                for t in range(4):
+                    nc.tensor.matmul(
+                        out=state["sxp"][:, 2 * b + h : 2 * b + h + 1],
+                        lhsT=x_sb[:, b, t, h * P : (h + 1) * P],
+                        rhs=ones_b[:],
+                        start=(t == 0),
+                        stop=(t == 3),
+                    )
+
+        def x_scale():
+            nc.vector.tensor_scalar_mul(out=sx01[:], in0=state["sxp"][:], scalar1=0.1)
 
         def ops(k):
             return state[("wc", k)], state[("ws", k)], state[("dc", k)], state[("ds", k)]
@@ -166,7 +219,7 @@ def tile_cssrclassifier_pa_kernel(tc, d, W_dec, x, out_0, out_1, out_2):
         def mm_a(k, i):
             bp, t = divmod(i, 4)
             wc, ws, dc, ds = ops(k)
-            pa = ps_a.tile([P, 512], F32, name="pa%d_%d" % (k, i), tag="aux")
+            pa = ps_a.tile([P, 512], F32, name="pa%d_%d" % (k, i), tag="pa")
             mc = slice(t * P, (t + 1) * P)
             ncol = slice(bp * 512, (bp + 1) * 512)
             nc.tensor.matmul_mx(
@@ -184,19 +237,26 @@ def tile_cssrclassifier_pa_kernel(tc, d, W_dec, x, out_0, out_1, out_2):
             bp, t = divmod(i, 4)
             if t == 0:
                 rec_new = recp.tile([P, 2, 4, NW], F32, name="rec%d_%d" % (k, bp), tag="rec")
-                state["rec"] = rec_new
-            rec = state["rec"]
-            nc.scalar.copy(out=rec[:, :, t, :], in_=state[("pa", k, i)][:].rearrange("p (b w) -> p b w", b=2))
+                state[("rec", k, bp)] = rec_new
+            rec = state[("rec", k, bp)]
+            o = rec[:, :, t, :]
+            s = state[("pa", k, i)][:].rearrange("p (b w) -> p b w", b=2)
+            if eng == "s":
+                nc.scalar.copy(out=o, in_=s)
+            else:
+                nc.vector.tensor_copy(out=o, in_=s)
             if t == 3:
-                eng.dma_start(
+                nc.sync.dma_start(
                     out=out_2[2 * bp : 2 * bp + 2, k].rearrange("b (p t) h w -> p b (t h w)", t=4),
                     in_=rec[:].rearrange("p b t w -> p b (t w)"),
                 )
+                if bp == 0 and k + AHEAD < NK:
+                    load_class(k + AHEAD)
 
         def mm_b(k, i):
             wc, ws, dc, ds = ops(k)
             mc = slice(i * P, (i + 1) * P)
-            pb = ps_b.tile([P, 512], F32, name="pb%d_%d" % (k, i), tag="aux")
+            pb = ps_b.tile([P, 512], F32, name="pb%d_%d" % (k, i), tag="pb")
             nc.tensor.matmul_mx(
                 out=pb[:],
                 lhsT=dc[:, mc].bitcast(FP8X4),
@@ -207,15 +267,15 @@ def tile_cssrclassifier_pa_kernel(tc, d, W_dec, x, out_0, out_1, out_2):
                 stop=True,
             )
             state[("pb", k, i)] = pb
-            g = i % 4
-            if g == 0:
-                pc_new = aux.tile([P, 4, P], F32, name="pc%d_%d" % (k, i), tag="aux")
-                state[("pc", k, i // 4)] = pc_new
-            pc = state[("pc", k, i // 4)]
+
+        def mm_c(k, i):
+            wc, ws, dc, ds = ops(k)
+            mc = slice(i * P, (i + 1) * P)
+            pc = ps_c.tile([P, P], F32, name="pc%d_%d" % (k, i), tag="pc")
             for t in range(4):
                 tcol = slice(t * P, (t + 1) * P)
                 nc.tensor.matmul_mx(
-                    out=pc[:, g, :],
+                    out=pc[:],
                     lhsT=dc[:, mc].bitcast(FP8X4),
                     lhsT_scale=ds[:, mc],
                     rhs=wc[:, tcol].bitcast(FP8X4),
@@ -223,6 +283,7 @@ def tile_cssrclassifier_pa_kernel(tc, d, W_dec, x, out_0, out_1, out_2):
                     start=(t == 0),
                     stop=(t == 3),
                 )
+            state[("pc", k, i)] = pc
 
         def col_of(k, i):
             return (i // 2) * 16 + k * 2 + (i % 2)
@@ -240,86 +301,139 @@ def tile_cssrclassifier_pa_kernel(tc, d, W_dec, x, out_0, out_1, out_2):
                 accum_out=smax[:, col : col + 1],
             )
 
-        def cacc(k, grp_i):
-            pc = state[("pc", k, grp_i)]
-            for gg in range(4):
-                col = col_of(k, grp_i * 4 + gg)
-                jc = junk.tile([P, P], BF16, name="jc%d_%d_%d" % (k, grp_i, gg), tag="jc")
-                nc.scalar.activation(
-                    out=jc[:], in_=pc[:, gg, :], func=ACT.Copy, scale=0.1, accum_out=sr01[:, col : col + 1]
-                )
+        def cacc(k, i):
+            col = col_of(k, i)
+            jc = junk.tile([P, P], BF16, name="jc%d_%d" % (k, i), tag="jc")
+            nc.scalar.activation(
+                out=jc[:], in_=state[("pc", k, i)][:], func=ACT.Copy, scale=0.1, accum_out=sr01[:, col : col + 1]
+            )
 
-        w_t(0)
-        w_exit(0, 0)
-        w_exit(0, 1)
-        x_tr(0)
-        x_tr(1)
-        x_exit(0)
-        x_exit(1)
-        rg_v(0, 0, 1)
-        rg_v(0, 1, 2)
-        q_w(0)
-        q_d(0, 0)
+        def program(first, steady, last):
+            ops = []
+            for k in range(NK):
+                for tok in (first if k == 0 else last if k == NK - 1 else steady).split(" "):
+                    if tok == "":
+                        continue
+                    kk = k + (1 if "+" in tok else 0)
+                    if kk < NK:
+                        ops.append((tok.replace("+", ""), kk))
+            return ops
 
-        for k in range(NK - 1):
-            for i in range(8):
-                mm_b(k, i)
-                mm_a(k, i)
-                stt(k, i)
-                copy_a(k, i, nc.gpsimd)
-                if k == 0:
-                    if i == 0:
-                        x_tr(2)
-                        x_tr(3)
-                        x_exit(2)
-                        rg_v(0, 2, 4)
-                    elif i == 1:
-                        x_exit(3)
-                    elif i == 2:
-                        q_d(0, 1)
-                    elif i == 3:
-                        nc.vector.tensor_scalar_mul(out=sx01[:], in0=sx[:], scalar1=0.1)
-                else:
-                    if i == 0:
-                        cacc(k - 1, 1)
-                    elif i == 1:
-                        q_d(k, 1)
-                if i == 1:
-                    w_t(k + 1)
-                elif i == 2:
-                    w_exit(k + 1, 0)
-                elif i == 3:
-                    w_exit(k + 1, 1)
-                    rg_v(k + 1, 0, 1)
-                elif i == 4:
-                    cacc(k, 0)
-                    rg_v(k + 1, 1, 2)
-                elif i == 5:
-                    rg_s(k + 1, 3, 0)
-                    q_w(k + 1)
-                elif i == 6:
-                    rg_s(k + 1, 3, 1)
-                    q_d(k + 1, 0)
-                elif i == 7:
-                    rg_v(k + 1, 2, 3)
+        progs = {
+            "PE": program(PE_FIRST, PE_STEADY, PE_LAST),
+            "V": program(V_FIRST, V_STEADY, V_LAST),
+            "S": program(S_FIRST, S_STEADY, S_LAST),
+            "G": program(G_FIRST, G_STEADY, G_LAST),
+        }
+        order = {}
+        done = set()
+        counts = {"tr": [], "r": []}
 
-        k = NK - 1
-        for g in range(4):
-            mm_b(k, 2 * g)
-            mm_b(k, 2 * g + 1)
-            mm_a(k, g)
-            stt(k, 2 * g)
-            stt(k, 2 * g + 1)
-            copy_a(k, g, nc.sync)
-            if g == 0:
-                cacc(k - 1, 1)
-                q_d(k, 1)
-            elif g == 2:
-                cacc(k, 0)
-        cacc(k, 1)
-        for i in range(4, 8):
-            mm_a(k, i)
-            copy_a(k, i, nc.scalar)
+        def imgs_ready(k, b):
+            return (("r%d" % b, k) in done) or (("r%da" % b, k) in done and ("r%db" % b, k) in done)
+
+        def ring(kind, k, i, bufs):
+            n = k * 8 + i - bufs
+            return n < 0 or (kind + str(n % 8), n // 8) in done
+
+        def quantised(k, i):
+            if ("W", k) not in done:
+                return False
+            if k == 0 and i < 4:
+                return ("d%d" % (i // 2), k) in done
+            return ("D%d" % (i // 4), k) in done
+
+        def ready(eng, op):
+            t, k = op
+            c = t[0]
+            if c in "TXY":
+                if c == "Y" and t != "Y0":
+                    return True
+                return len(counts["tr"]) < WT or counts["tr"][-WT] in done
+            if c == "b":
+                return quantised(k, int(t[1])) and ring("s", k, int(t[1]), PB)
+            if c == "c":
+                return quantised(k, int(t[1])) and ring("C", k, int(t[1]), PCB)
+            if c == "a":
+                i = int(t[1])
+                return ("W", k) in done and (
+                    (("d0", k) in done and ("d1", k) in done) if k == 0 and i < 4 else ("D%d" % (i // 4), k) in done
+                ) and ring("A", k, i, PA)
+            if t == "xs":
+                return ("Y3", NK - 1) in done
+            if c == "s":
+                return ("b" + t[1], k) in done and ("x%d" % (int(t[1]) // 2), 0) in done
+            if c == "C":
+                return ("c" + t[1], k) in done
+            if c == "A":
+                return ("a" + t[1], k) in done
+            if c == "e":
+                return ("T" + t[1], k) in done
+            if c == "x":
+                return ("X" + t[1], k) in done
+            if c == "W":
+                return ("e0", k) in done and ("e1", k) in done
+            if c == "D":
+                return imgs_ready(k, 2 * int(t[1])) and imgs_ready(k, 2 * int(t[1]) + 1)
+            if c == "d":
+                return imgs_ready(k, int(t[1]))
+            if c == "r":
+                p = int(t[1]) // 2
+                return k < GRP or ("D%d" % p, k - GRP) in done or (k == GRP and p == 0 and ("d1", 0) in done)
+            return True
+
+        def emit(eng, op):
+            t, k = op
+            c = t[0]
+            n = 0 if t in ("W", "xs") else int(t[1])
+            if c == "T":
+                w_t(k, n)
+                counts["tr"].append(("e%d" % n, k))
+            elif c == "X":
+                x_tr(n)
+                counts["tr"].append(("x%d" % n, 0))
+            elif c == "Y":
+                x_sum(n)
+                if n == 0:
+                    counts["tr"].append(("xs", NK - 1))
+            elif c == "b":
+                mm_b(k, n)
+            elif c == "c":
+                mm_c(k, n)
+            elif c == "a":
+                mm_a(k, n)
+            elif t == "xs":
+                x_scale()
+            elif c == "s":
+                stt(k, n)
+            elif c == "C":
+                cacc(k, n)
+            elif c == "A":
+                copy_a(k, n, "s" if eng == "S" else "v")
+            elif c == "e":
+                w_exit(k, n, "s" if eng == "S" else "v")
+            elif c == "x":
+                x_exit(n, "s" if eng == "S" else "v")
+            elif c == "W":
+                q_w(k)
+            elif c == "D":
+                q_d(k, n)
+            elif c == "d":
+                q_d_cols(k, n, n + 1)
+            elif c == "r":
+                half = {"a": (0, 1), "b": (1, 2)}.get(t[2:3], (0, 2))
+                rg(k, n, half[0], half[1], eng)
+            done.add((t, k))
+
+        left = {e: list(p) for e, p in progs.items()}
+        while any(left.values()):
+            moved = False
+            for e in ("PE", "V", "S", "G"):
+                while left[e] and ready(e, left[e][0]):
+                    emit(e, left[e][0])
+                    left[e] = left[e][1:]
+                    moved = True
+            assert moved, str({e: p[:2] for e, p in left.items()})
 
         def v4(ap):
             return ap.rearrange("p (b k h) -> p b k h", b=NB, k=NK, h=2)
@@ -345,21 +459,18 @@ def tile_cssrclassifier_pa_kernel(tc, d, W_dec, x, out_0, out_1, out_2):
         nc.vector.tensor_tensor(out=v4(sh[:]), in0=v4(lg[:]), in1=bc(mxk[:]), op=ALU.subtract)
         ex = const.tile([P, 64], F32)
         nc.scalar.activation(out=ex[:], in_=sh[:], func=ACT.Exp)
+        lsum = const.tile([P, 32], F32)
+        lg3 = lg[:].rearrange("p (c h) -> p c h", h=2)
+        nc.vector.tensor_tensor(out=lsum[:], in0=lg3[:, :, 0], in1=lg3[:, :, 1], op=ALU.add)
+        pmean = ps_t.tile([P, 32], F32, name="pmean", tag="tr")
+        nc.tensor.matmul(out=pmean[:], lhsT=ones_f[:], rhs=lsum[:], start=True, stop=True)
         den = const.tile([P, 8], F32)
         nc.vector.tensor_reduce(out=groups(den[:]), in_=by_group(ex[:]), axis=AX.X, op=ALU.add)
         rden = const.tile([P, 8], F32)
         nc.vector.reciprocal(out=rden[:], in_=den[:])
         nc.vector.tensor_tensor(out=v4(pad[:, 0:64]), in0=v4(ex[:]), in1=bc(rden[:]), op=ALU.mult)
-        pt = aux.tile([P, P], F32, name="pt", tag="aux")
+        pt = ps_t.tile([P, P], F32, name="pt", tag="tr")
         nc.tensor.transpose(pt[:], pad[:], ident_f[:])
-        lsum = const.tile([P, 32], F32)
-        lg3 = lg[:].rearrange("p (c h) -> p c h", h=2)
-        nc.vector.tensor_tensor(out=lsum[:], in0=lg3[:, :, 0], in1=lg3[:, :, 1], op=ALU.add)
-        pmean = aux.tile([P, 32], F32, name="pmean", tag="aux")
-        nc.tensor.matmul(out=pmean[:], lhsT=ones_f[:], rhs=lsum[:], start=True, stop=True)
-        p_out = const.tile([P, P], F32)
-        nc.vector.tensor_copy(out=p_out[:], in_=pt[:])
-        nc.sync.dma_start(out=out_0.rearrange("b k (h r) w -> (b k h) (r w)", h=2), in_=p_out[0:64, :])
         e_sel = const.tile([P, NB, NK], F32)
         nc.vector.tensor_tensor(
             out=e_sel[:],
@@ -370,3 +481,6 @@ def tile_cssrclassifier_pa_kernel(tc, d, W_dec, x, out_0, out_1, out_2):
         e_out = const.tile([P, NK], F32)
         nc.vector.tensor_reduce(out=e_out[:], in_=e_sel[:].rearrange("p b k -> p k b"), axis=AX.X, op=ALU.add)
         nc.sync.dma_start(out=out_1, in_=e_out[0:NB, :])
+        p_out = const.tile([P, P], F32)
+        nc.vector.tensor_copy(out=p_out[:], in_=pt[:])
+        nc.sync.dma_start(out=out_0.rearrange("b k (h r) w -> (b k h) (r w)", h=2), in_=p_out[0:64, :])

@@ -17,19 +17,22 @@ NK, NB, NC, NJ, NW = 8, 4, 512, 512, 256
 FLOPS = 2 * NK * NB * NC * NJ * NW
 
 GRP = 2
+GRP1 = 2
+ABS = ()
 AHEAD = 4
 MANUAL = True
-PA, PB, PCB, WT = 2, 2, 2, 2
-PE_FIRST = "T0 T1 X0 b0 b1 X1 c0 b2 c1 a0 a1 X2 X3 b3 c2 a2 T0+ T1+ b4 c3 a3 b5 c4 a4 b6 c5 a5 b7 c6 a6 b0+ c7 a7"
-PE_STEADY = "b1 c0 a0 b2 c1 a1 T0+ T1+ b3 c2 a2 b4 c3 a3 b5 c4 a4 b6 c5 a5 b7 c6 a6 b0+ c7 a7"
-V_FIRST = "r0 W d0 r1 s0 d1 s1 r2 s2 r3 s3 D1 r0+ s4 r1+ s5 W+ s6 D0+ s7 r2+"
-V_STEADY = "s0 D1 s1 r0+ s2 r1+ s3 r2+ s4 s5 W+ s6 D0+ s7"
-S_FIRST = "e0 e1 x0 x1 C0 A0 x2 C1 A1 x3 C2 A2 e0+ e1+ C3 A3 C4 A4 C5 A5 C6 A6 C7 r3a+ A7 r3b+"
-S_STEADY = "C0 A0 C1 A1 e0+ C2 A2 e1+ C3 A3 C4 A4 r3a+ C5 A5 r3b+ C6 A6 C7 A7"
-PE_LAST = "b1 c0 a0 Y0 Y1 Y2 Y3 b2 c1 a1 b3 c2 a2 b4 c3 a3 b5 c4 b6 c5 b7 c6 c7 a4 a5 a6 a7"
-V_LAST = "s0 D1 s1 xs s2 s3 s4 s5 s6 s7"
-S_LAST = "C0 A0 C1 A1 C2 A2 C3 A3 C4 C5 C6 C7 A4 A5 A6 A7"
+BANKS = 8
+PE_FIRST = "T0 T1 X0 b0 b1 X1 b2 c0 c1 b3 a0 a1 X2 X3 c2 c3 T0+ T1+ b4 b5 a2 a3 c4 a4 b6 c5 a5 b7 c6 a6 b0+ b1+ c7 a7"
+PE_STEADY = "c0 a0 c1 a1 b2 b3 T0+ T1+ c2 a2 c3 a3 b4 b5 c4 a4 c5 a5 b6 b7 c6 a6 c7 a7 b0+ b1+"
+V_FIRST = "r0 W d0 r1 s0 d1 s1 r2 s2 r3 s3 D1 r0p+ s5 s4 W+ s6 D0+ s7 r2+"
+V_STEADY = "s1 s0 D1 r0p+ s3 s2 r2+ s5 s4 W+ D0+ s7 s6"
+S_FIRST = "e0 e1 x0 x1 A0 A1 x2 x3 e0+ e1+ A2 A3 C3 C2 C1 C0 A4 A5 r3+ A6 C7 C6 C5 C4 A7"
+S_STEADY = "A0 A1 e0+ A2 e1+ C3 C2 C1 C0 A3 r3+ A4 A5 A6 A7 C7 C6 C5 C4"
+PE_LAST = "c0 a0 b2 b3 c1 a1 c2 c3 b4 b5 a2 b6 b7 c4 c5 c6 c7 a3 a4 a5 a6 a7"
+V_LAST = "s1 s0 D1 xs s3 s2 s5 s4 s7 s6"
+S_LAST = "A0 A1 C3 C2 C1 C0 A2 C7 C6 C5 C4 A3 A4 A5"
 G_LAST = ""
+S_TAIL = "A6 A7"
 G_FIRST = ""
 G_STEADY = ""
 
@@ -42,16 +45,14 @@ def tile_cssrclassifier_pa_kernel(tc, d, W_dec, x, out_0, out_1, out_2):
         grp = ctx.enter_context(tc.tile_pool(name="grp", bufs=GRP))
         mx = ctx.enter_context(tc.tile_pool(name="mx", bufs=3))
         recp = ctx.enter_context(tc.tile_pool(name="recp", bufs=6))
-        junk = ctx.enter_context(tc.tile_pool(name="junk", bufs=2))
-        ps_a = ctx.enter_context(tc.psum_pool(name="ps_a", bufs=PA))
-        ps_b = ctx.enter_context(tc.psum_pool(name="ps_b", bufs=PB))
-        ps_c = ctx.enter_context(tc.psum_pool(name="ps_c", bufs=PCB))
-        ps_t = ctx.enter_context(tc.psum_pool(name="ps_t", bufs=WT))
+        junk = ctx.enter_context(tc.tile_pool(name="junk", bufs=4))
+        psum = ctx.enter_context(tc.psum_pool(name="psum", bufs=BANKS))
         if MANUAL:
             ctx.enter_context(tc.manual_schedule())
 
         smax = const.tile([P, 64], F32)
         sr01 = const.tile([P, 64], F32)
+        sx = const.tile([P, 8], F32)
         sx01 = const.tile([P, 8], F32)
         x_sb = const.tile([P, NB, 4, NW], BF16)
         x_t = const.tile([P, 8, NC], BF16)
@@ -100,8 +101,6 @@ def tile_cssrclassifier_pa_kernel(tc, d, W_dec, x, out_0, out_1, out_2):
         make_identity(nc, ident_f[:])
         ident_b = const.tile([P, P], BF16)
         make_identity(nc, ident_b[:])
-        ones_b = const.tile([P, 1], BF16)
-        nc.vector.memset(ones_b[:], 1.0)
         warm = const.tile([P, 1], F32)
         nc.vector.memset(warm[:], 0.0)
         warm2 = const.tile([P, 1], F32)
@@ -113,7 +112,7 @@ def tile_cssrclassifier_pa_kernel(tc, d, W_dec, x, out_0, out_1, out_2):
 
         def w_t(k, g):
             wf = state[("w_raw", k)][:].bitcast(F32)
-            wt = ps_t.tile([P, 4, P], F32, name="wt%d_%d" % (k, g), tag="tr")
+            wt = psum.tile([P, 4, P], F32, name="wt%d_%d" % (k, g), tag="bank")
             for tt in range(2):
                 for u in range(2):
                     nc.tensor.transpose(wt[:, tt * 2 + u, :], wf[:, 2 * g + tt, u : 2 * P : 2], ident_f[:])
@@ -142,11 +141,11 @@ def tile_cssrclassifier_pa_kernel(tc, d, W_dec, x, out_0, out_1, out_2):
         def dg_of(k, b):
             key = ("dg", k, b // 2)
             if key not in state:
-                dg_new = grp.tile([P, 2, NW, 4], BF16, name="dg%d_%d" % (k, b // 2), tag="dg%d" % (b // 2), align_bytes=64)
+                dg_new = grp.tile([P, 2, NW, 4], BF16, name="dg%d_%d" % (k, b // 2), tag="dg%d" % (b // 2), align_bytes=64, bufs=GRP if b < 2 else GRP1)
                 state[key] = dg_new
             return state[key]
 
-        def rg(k, b, h0, h1, eng):
+        def rg(k, b, n, h0, h1, eng):
             if eng == "G":
                 ws = slice(h0 * NW // 2, h1 * NW // 2)
                 nc.gpsimd.tensor_scalar(
@@ -159,8 +158,12 @@ def tile_cssrclassifier_pa_kernel(tc, d, W_dec, x, out_0, out_1, out_2):
                 )
                 return
             cs = slice(h0 * 32, h1 * 32)
-            src = state[("d_raw", k)][:, b].rearrange("q t (c i) -> q c t i", i=4)[:, cs]
-            dst = dg_of(k, b)[:, b % 2].rearrange("q (c i) t -> q c t i", i=4)[:, cs]
+            if n == 2:
+                src = state[("d_raw", k)][:, b : b + 2].rearrange("q b t (c i) -> q b c t i", i=4)
+                dst = dg_of(k, b)[:].rearrange("q b (c i) t -> q b c t i", i=4)
+            else:
+                src = state[("d_raw", k)][:, b].rearrange("q t (c i) -> q c t i", i=4)[:, cs]
+                dst = dg_of(k, b)[:, b % 2].rearrange("q (c i) t -> q c t i", i=4)[:, cs]
             if eng == "V":
                 nc.vector.tensor_copy(out=dst, in_=src)
             else:
@@ -183,35 +186,29 @@ def tile_cssrclassifier_pa_kernel(tc, d, W_dec, x, out_0, out_1, out_2):
             q_d_cols(k, 2 * bp, 2 * bp + 2)
 
         def x_tr(b):
-            xp = ps_t.tile([P, 2, NC], BF16, name="xp%d" % b, tag="tr")
+            xp = psum.tile([P, 2, NC], BF16, name="xp%d" % b, tag="bank")
             for h in range(2):
                 for t in range(4):
                     nc.tensor.transpose(xp[:, h, t * P : (t + 1) * P], x_sb[:, b, t, h * P : (h + 1) * P], ident_b[:])
             state[("xp", b)] = xp
 
-        def x_exit(b, eng="s"):
+        def x_exit(b):
             xp = state[("xp", b)]
-            o = x_t[:, 2 * b : 2 * b + 2, :]
-            if eng == "s":
-                nc.scalar.copy(out=o, in_=xp[:])
-            else:
-                nc.vector.tensor_copy(out=o, in_=xp[:])
-
-        def x_sum(b):
-            if b == 0:
-                state["sxp"] = ps_t.tile([P, 8], F32, name="sxp", tag="tr")
             for h in range(2):
-                for t in range(4):
-                    nc.tensor.matmul(
-                        out=state["sxp"][:, 2 * b + h : 2 * b + h + 1],
-                        lhsT=x_sb[:, b, t, h * P : (h + 1) * P],
-                        rhs=ones_b[:],
-                        start=(t == 0),
-                        stop=(t == 3),
-                    )
+                i = 2 * b + h
+                nc.scalar.activation(out=x_t[:, i, :], in_=xp[:, h, :], func=ACT.Copy, accum_out=sx[:, i : i + 1])
 
         def x_scale():
-            nc.vector.tensor_scalar_mul(out=sx01[:], in0=state["sxp"][:], scalar1=0.1)
+            if not ABS:
+                nc.vector.tensor_scalar_mul(out=sx01[:], in0=sx[:], scalar1=0.1)
+                return
+            for i in range(8):
+                if i in ABS:
+                    nc.vector.memset(sx01[:, i : i + 1], 0.0)
+                    for k in range(NK):
+                        nc.vector.memset(sr01[:, col_of(k, i) : col_of(k, i) + 1], 0.0)
+                else:
+                    nc.vector.tensor_scalar_mul(out=sx01[:, i : i + 1], in0=sx[:, i : i + 1], scalar1=0.1)
 
         def ops(k):
             return state[("wc", k)], state[("ws", k)], state[("dc", k)], state[("ds", k)]
@@ -219,7 +216,7 @@ def tile_cssrclassifier_pa_kernel(tc, d, W_dec, x, out_0, out_1, out_2):
         def mm_a(k, i):
             bp, t = divmod(i, 4)
             wc, ws, dc, ds = ops(k)
-            pa = ps_a.tile([P, 512], F32, name="pa%d_%d" % (k, i), tag="pa")
+            pa = psum.tile([P, 512], F32, name="pa%d_%d" % (k, i), tag="bank")
             mc = slice(t * P, (t + 1) * P)
             ncol = slice(bp * 512, (bp + 1) * 512)
             nc.tensor.matmul_mx(
@@ -235,20 +232,24 @@ def tile_cssrclassifier_pa_kernel(tc, d, W_dec, x, out_0, out_1, out_2):
 
         def copy_a(k, i, eng):
             bp, t = divmod(i, 4)
-            if t == 0:
-                rec_new = recp.tile([P, 2, 4, NW], F32, name="rec%d_%d" % (k, bp), tag="rec")
-                state[("rec", k, bp)] = rec_new
-            rec = state[("rec", k, bp)]
-            o = rec[:, :, t, :]
+            n = 2 if k == NK - 1 and bp == 1 else 4
+            key = ("rec", k, bp, t // n)
+            if key not in state:
+                rec_new = recp.tile([P, 2, n, NW], F32, name="rec%d_%d_%d" % (k, bp, t // n), tag="rec")
+                state[key] = [rec_new, 0]
+            rec = state[key][0]
+            o = rec[:, :, t % n, :]
             s = state[("pa", k, i)][:].rearrange("p (b w) -> p b w", b=2)
             if eng == "s":
                 nc.scalar.copy(out=o, in_=s)
             else:
                 nc.vector.tensor_copy(out=o, in_=s)
-            if t == 3:
+            state[key][1] += 1
+            if state[key][1] == n:
+                t0 = t // n * n
                 nc.sync.dma_start(
-                    out=out_2[2 * bp : 2 * bp + 2, k].rearrange("b (p t) h w -> p b (t h w)", t=4),
-                    in_=rec[:].rearrange("p b t w -> p b (t w)"),
+                    out=out_2[2 * bp : 2 * bp + 2, k].rearrange("b (p t) h w -> p b t (h w)", t=4)[:, :, t0 : t0 + n],
+                    in_=rec[:],
                 )
                 if bp == 0 and k + AHEAD < NK:
                     load_class(k + AHEAD)
@@ -256,7 +257,7 @@ def tile_cssrclassifier_pa_kernel(tc, d, W_dec, x, out_0, out_1, out_2):
         def mm_b(k, i):
             wc, ws, dc, ds = ops(k)
             mc = slice(i * P, (i + 1) * P)
-            pb = ps_b.tile([P, 512], F32, name="pb%d_%d" % (k, i), tag="pb")
+            pb = psum.tile([P, 512], F32, name="pb%d_%d" % (k, i), tag="bank")
             nc.tensor.matmul_mx(
                 out=pb[:],
                 lhsT=dc[:, mc].bitcast(FP8X4),
@@ -271,11 +272,14 @@ def tile_cssrclassifier_pa_kernel(tc, d, W_dec, x, out_0, out_1, out_2):
         def mm_c(k, i):
             wc, ws, dc, ds = ops(k)
             mc = slice(i * P, (i + 1) * P)
-            pc = ps_c.tile([P, P], F32, name="pc%d_%d" % (k, i), tag="pc")
+            if ("pc", k, i // 4) not in state:
+                pc_new = psum.tile([P, 4, P], F32, name="pc%d_%d" % (k, i), tag="bank")
+                state[("pc", k, i // 4)] = pc_new
+            pc = state[("pc", k, i // 4)]
             for t in range(4):
                 tcol = slice(t * P, (t + 1) * P)
                 nc.tensor.matmul_mx(
-                    out=pc[:],
+                    out=pc[:, i % 4, :],
                     lhsT=dc[:, mc].bitcast(FP8X4),
                     lhsT_scale=ds[:, mc],
                     rhs=wc[:, tcol].bitcast(FP8X4),
@@ -283,7 +287,6 @@ def tile_cssrclassifier_pa_kernel(tc, d, W_dec, x, out_0, out_1, out_2):
                     start=(t == 0),
                     stop=(t == 3),
                 )
-            state[("pc", k, i)] = pc
 
         def col_of(k, i):
             return (i // 2) * 16 + k * 2 + (i % 2)
@@ -301,11 +304,23 @@ def tile_cssrclassifier_pa_kernel(tc, d, W_dec, x, out_0, out_1, out_2):
                 accum_out=smax[:, col : col + 1],
             )
 
+        def diff(k, i):
+            df = junk.tile([P, 512], F32, name="df%d_%d" % (k, i), tag="df")
+            nc.vector.tensor_tensor(out=df[:], in0=state[("pb", k, i)][:], in1=x_t[:, i, :], op=ALU.subtract)
+            state[("df", k, i)] = df
+
+        def absacc(k, i):
+            col = col_of(k, i)
+            ja = junk.tile([P, 512], BF16, name="ja%d_%d" % (k, i), tag="ja")
+            nc.scalar.activation(
+                out=ja[:], in_=state[("df", k, i)][:], func=ACT.Abs, scale=0.5, accum_out=smax[:, col : col + 1]
+            )
+
         def cacc(k, i):
             col = col_of(k, i)
             jc = junk.tile([P, P], BF16, name="jc%d_%d" % (k, i), tag="jc")
             nc.scalar.activation(
-                out=jc[:], in_=state[("pc", k, i)][:], func=ACT.Copy, scale=0.1, accum_out=sr01[:, col : col + 1]
+                out=jc[:], in_=state[("pc", k, i // 4)][:, i % 4, :], func=ACT.Copy, scale=0.1, accum_out=sr01[:, col : col + 1]
             )
 
         def program(first, steady, last):
@@ -327,14 +342,10 @@ def tile_cssrclassifier_pa_kernel(tc, d, W_dec, x, out_0, out_1, out_2):
         }
         order = {}
         done = set()
-        counts = {"tr": [], "r": []}
+        live = [0]
 
         def imgs_ready(k, b):
             return (("r%d" % b, k) in done) or (("r%da" % b, k) in done and ("r%db" % b, k) in done)
-
-        def ring(kind, k, i, bufs):
-            n = k * 8 + i - bufs
-            return n < 0 or (kind + str(n % 8), n // 8) in done
 
         def quantised(k, i):
             if ("W", k) not in done:
@@ -346,25 +357,25 @@ def tile_cssrclassifier_pa_kernel(tc, d, W_dec, x, out_0, out_1, out_2):
         def ready(eng, op):
             t, k = op
             c = t[0]
-            if c in "TXY":
-                if c == "Y" and t != "Y0":
-                    return True
-                return len(counts["tr"]) < WT or counts["tr"][-WT] in done
-            if c == "b":
-                return quantised(k, int(t[1])) and ring("s", k, int(t[1]), PB)
-            if c == "c":
-                return quantised(k, int(t[1])) and ring("C", k, int(t[1]), PCB)
+            if (c in "TXba" or t in ("c0", "c4")) and live[0] == BANKS:
+                return False
+            if c in "TX":
+                return True
+            if c in "bc":
+                return quantised(k, int(t[1]))
             if c == "a":
                 i = int(t[1])
                 return ("W", k) in done and (
                     (("d0", k) in done and ("d1", k) in done) if k == 0 and i < 4 else ("D%d" % (i // 4), k) in done
-                ) and ring("A", k, i, PA)
+                )
             if t == "xs":
-                return ("Y3", NK - 1) in done
+                return ("x3", 0) in done
             if c == "s":
                 return ("b" + t[1], k) in done and ("x%d" % (int(t[1]) // 2), 0) in done
             if c == "C":
-                return ("c" + t[1], k) in done
+                return all([("c%d" % j, k) in done for j in range(int(t[1]) // 4 * 4, int(t[1]) // 4 * 4 + 4) if j not in ABS])
+            if c == "Z":
+                return ("s" + t[1], k) in done
             if c == "A":
                 return ("a" + t[1], k) in done
             if c == "e":
@@ -379,7 +390,8 @@ def tile_cssrclassifier_pa_kernel(tc, d, W_dec, x, out_0, out_1, out_2):
                 return imgs_ready(k, int(t[1]))
             if c == "r":
                 p = int(t[1]) // 2
-                return k < GRP or ("D%d" % p, k - GRP) in done or (k == GRP and p == 0 and ("d1", 0) in done)
+                g = GRP if p == 0 else GRP1
+                return k < g or ("D%d" % p, k - g) in done or (k == g and p == 0 and ("d1", 0) in done)
             return True
 
         def emit(eng, op):
@@ -388,14 +400,8 @@ def tile_cssrclassifier_pa_kernel(tc, d, W_dec, x, out_0, out_1, out_2):
             n = 0 if t in ("W", "xs") else int(t[1])
             if c == "T":
                 w_t(k, n)
-                counts["tr"].append(("e%d" % n, k))
             elif c == "X":
                 x_tr(n)
-                counts["tr"].append(("x%d" % n, 0))
-            elif c == "Y":
-                x_sum(n)
-                if n == 0:
-                    counts["tr"].append(("xs", NK - 1))
             elif c == "b":
                 mm_b(k, n)
             elif c == "c":
@@ -405,7 +411,12 @@ def tile_cssrclassifier_pa_kernel(tc, d, W_dec, x, out_0, out_1, out_2):
             elif t == "xs":
                 x_scale()
             elif c == "s":
-                stt(k, n)
+                if n in ABS:
+                    diff(k, n)
+                else:
+                    stt(k, n)
+            elif c == "Z":
+                absacc(k, n)
             elif c == "C":
                 cacc(k, n)
             elif c == "A":
@@ -413,7 +424,7 @@ def tile_cssrclassifier_pa_kernel(tc, d, W_dec, x, out_0, out_1, out_2):
             elif c == "e":
                 w_exit(k, n, "s" if eng == "S" else "v")
             elif c == "x":
-                x_exit(n, "s" if eng == "S" else "v")
+                x_exit(n)
             elif c == "W":
                 q_w(k)
             elif c == "D":
@@ -422,7 +433,14 @@ def tile_cssrclassifier_pa_kernel(tc, d, W_dec, x, out_0, out_1, out_2):
                 q_d_cols(k, n, n + 1)
             elif c == "r":
                 half = {"a": (0, 1), "b": (1, 2)}.get(t[2:3], (0, 2))
-                rg(k, n, half[0], half[1], eng)
+                rg(k, n, 2 if t[2:3] == "p" else 1, half[0], half[1], eng)
+                if t[2:3] == "p":
+                    done.add(("r%d" % n, k))
+                    done.add(("r%d" % (n + 1), k))
+            if c in "TXba" or t in ("c0", "c4"):
+                live[0] += 1
+            elif c in "esA" or t in ("C0", "C4") or (c == "x" and t != "xs"):
+                live[0] -= 1
             done.add((t, k))
 
         left = {e: list(p) for e, p in progs.items()}
@@ -459,17 +477,19 @@ def tile_cssrclassifier_pa_kernel(tc, d, W_dec, x, out_0, out_1, out_2):
         nc.vector.tensor_tensor(out=v4(sh[:]), in0=v4(lg[:]), in1=bc(mxk[:]), op=ALU.subtract)
         ex = const.tile([P, 64], F32)
         nc.scalar.activation(out=ex[:], in_=sh[:], func=ACT.Exp)
+        for tok in S_TAIL.split(" "):
+            emit("S", (tok, NK - 1))
         lsum = const.tile([P, 32], F32)
         lg3 = lg[:].rearrange("p (c h) -> p c h", h=2)
         nc.vector.tensor_tensor(out=lsum[:], in0=lg3[:, :, 0], in1=lg3[:, :, 1], op=ALU.add)
-        pmean = ps_t.tile([P, 32], F32, name="pmean", tag="tr")
+        pmean = psum.tile([P, 32], F32, name="pmean", tag="bank")
         nc.tensor.matmul(out=pmean[:], lhsT=ones_f[:], rhs=lsum[:], start=True, stop=True)
         den = const.tile([P, 8], F32)
         nc.vector.tensor_reduce(out=groups(den[:]), in_=by_group(ex[:]), axis=AX.X, op=ALU.add)
         rden = const.tile([P, 8], F32)
         nc.vector.reciprocal(out=rden[:], in_=den[:])
         nc.vector.tensor_tensor(out=v4(pad[:, 0:64]), in0=v4(ex[:]), in1=bc(rden[:]), op=ALU.mult)
-        pt = ps_t.tile([P, P], F32, name="pt", tag="tr")
+        pt = psum.tile([P, P], F32, name="pt", tag="bank")
         nc.tensor.transpose(pt[:], pad[:], ident_f[:])
         e_sel = const.tile([P, NB, NK], F32)
         nc.vector.tensor_tensor(

@@ -17,24 +17,24 @@ NK, NB, NC, NJ, NW = 8, 4, 512, 512, 256
 FLOPS = 2 * NK * NB * NC * NJ * NW
 
 GRP = 2
-GRP1 = 2
-ABS = ()
+GRP1 = 1
+ABS = (6, 7)
 AHEAD = 4
 MANUAL = True
 BANKS = 8
-PE_FIRST = "T0 T1 X0 b0 b1 X1 b2 c0 c1 b3 a0 a1 X2 X3 c2 c3 T0+ T1+ b4 b5 a2 a3 c4 a4 b6 c5 a5 b7 c6 a6 b0+ b1+ c7 a7"
-PE_STEADY = "c0 a0 c1 a1 b2 b3 T0+ T1+ c2 a2 c3 a3 b4 b5 c4 a4 c5 a5 b6 b7 c6 a6 c7 a7 b0+ b1+"
-V_FIRST = "r0 W d0 r1 s0 d1 s1 r2 s2 r3 s3 D1 r0p+ s5 s4 W+ s6 D0+ s7 r2+"
-V_STEADY = "s1 s0 D1 r0p+ s3 s2 r2+ s5 s4 W+ D0+ s7 s6"
-S_FIRST = "e0 e1 x0 x1 A0 A1 x2 x3 e0+ e1+ A2 A3 C3 C2 C1 C0 A4 A5 r3+ A6 C7 C6 C5 C4 A7"
-S_STEADY = "A0 A1 e0+ A2 e1+ C3 C2 C1 C0 A3 r3+ A4 A5 A6 A7 C7 C6 C5 C4"
+PE_FIRST = "T0 T1 X0 b0 b1 X1 b2 c0 c1 b3 a0 a1 X2 X3 c2 c3 b4 b5 T0+ T1+ a2 a3 c4 a4 b6 c5 a5 b7 a6 b0+ b1+ a7"
+PE_STEADY = "b2 b3 c0 c1 a0 b4 b5 a1 T0+ T1+ c2 c3 a2 a3 b6 b7 c4 c5 a4 a5 b0+ b1+ a6 a7"
+V_FIRST = "r0 W d0 r1 s0 d1 s1 r2 s2 r3 s3 D1 r0p+ s5 s4 W+ D0+ xs s7 r2+ s6"
+V_STEADY = "D1 s1 s0 s3 s2 s5 s4 r0p+ W+ D0+ s7 s6"
+S_FIRST = "e0 e1 x0 x1 A0 A1 x2 x3 e0+ e1+ A2 A3 C3 C2 C1 C0 A4 A5 r3+ A6 C5 C4 Z7 Z6 A7"
+S_STEADY = "A0 A1 e0+ e1+ A2 C3 C2 C1 C0 A3 A4 A5 C5 C4 A6 Z7 Z6 A7"
 PE_LAST = "c0 a0 b2 b3 c1 a1 c2 c3 b4 b5 a2 b6 b7 c4 c5 c6 c7 a3 a4 a5 a6 a7"
-V_LAST = "s1 s0 D1 xs s3 s2 s5 s4 s7 s6"
+V_LAST = "D1 s1 s0 s3 s2 s5 s4 s7 s6"
 S_LAST = "A0 A1 C3 C2 C1 C0 A2 C7 C6 C5 C4 A3 A4 A5"
 G_LAST = ""
 S_TAIL = "A6 A7"
 G_FIRST = ""
-G_STEADY = ""
+G_STEADY = "r2+ r3+"
 
 
 def tile_cssrclassifier_pa_kernel(tc, d, W_dec, x, out_0, out_1, out_2):
@@ -199,16 +199,19 @@ def tile_cssrclassifier_pa_kernel(tc, d, W_dec, x, out_0, out_1, out_2):
                 nc.scalar.activation(out=x_t[:, i, :], in_=xp[:, h, :], func=ACT.Copy, accum_out=sx[:, i : i + 1])
 
         def x_scale():
-            if not ABS:
-                nc.vector.tensor_scalar_mul(out=sx01[:], in0=sx[:], scalar1=0.1)
-                return
-            for i in range(8):
-                if i in ABS:
-                    nc.vector.memset(sx01[:, i : i + 1], 0.0)
-                    for k in range(NK):
-                        nc.vector.memset(sr01[:, col_of(k, i) : col_of(k, i) + 1], 0.0)
-                else:
-                    nc.vector.tensor_scalar_mul(out=sx01[:, i : i + 1], in0=sx[:, i : i + 1], scalar1=0.1)
+            nc.vector.tensor_scalar_mul(out=sx01[:], in0=sx[:], scalar1=0.1)
+            if ABS:
+                i0 = ABS[0]
+                n = len(ABS)
+                dst = sr01[:, i0 // 2 * 16 : i0 // 2 * 16 + 2 * (NK - 1)].rearrange("p (k h) -> p h k", h=2)
+                nc.vector.tensor_scalar_mul(
+                    out=dst[:, 2 - n : 2],
+                    in0=sx01[:, i0 : i0 + n].unsqueeze(2).to_broadcast([P, n, NK - 1]),
+                    scalar1=-1.0,
+                )
+
+        def direct(k, i):
+            return i in ABS and k < NK - 1
 
         def ops(k):
             return state[("wc", k)], state[("ws", k)], state[("dc", k)], state[("ds", k)]
@@ -373,7 +376,7 @@ def tile_cssrclassifier_pa_kernel(tc, d, W_dec, x, out_0, out_1, out_2):
             if c == "s":
                 return ("b" + t[1], k) in done and ("x%d" % (int(t[1]) // 2), 0) in done
             if c == "C":
-                return all([("c%d" % j, k) in done for j in range(int(t[1]) // 4 * 4, int(t[1]) // 4 * 4 + 4) if j not in ABS])
+                return all([("c%d" % j, k) in done for j in range(int(t[1]) // 4 * 4, int(t[1]) // 4 * 4 + 4) if not direct(k, j)])
             if c == "Z":
                 return ("s" + t[1], k) in done
             if c == "A":
@@ -411,7 +414,7 @@ def tile_cssrclassifier_pa_kernel(tc, d, W_dec, x, out_0, out_1, out_2):
             elif t == "xs":
                 x_scale()
             elif c == "s":
-                if n in ABS:
+                if direct(k, n):
                     diff(k, n)
                 else:
                     stt(k, n)

@@ -18,23 +18,23 @@ FLOPS = 2 * NK * NB * NC * NJ * NW
 
 GRP = 2
 GRP1 = 1
-ABS = (6, 7)
+ABS = (7,)
 AHEAD = 4
 MANUAL = True
 BANKS = 8
-PE_FIRST = "T0 T1 X0 b0 b1 X1 b2 c0 c1 b3 a0 a1 X2 X3 c2 c3 b4 b5 T0+ T1+ a2 a3 c4 a4 b6 c5 a5 b7 a6 b0+ b1+ a7"
-PE_STEADY = "b2 b3 c0 c1 a0 b4 b5 a1 T0+ T1+ c2 c3 a2 a3 b6 b7 c4 c5 a4 a5 b0+ b1+ a6 a7"
-V_FIRST = "r0 W d0 r1 s0 d1 s1 r2 s2 r3 s3 D1 r0p+ s5 s4 W+ D0+ xs s7 r2+ s6"
-V_STEADY = "D1 s1 s0 s3 s2 s5 s4 r0p+ W+ D0+ s7 s6"
-S_FIRST = "e0 e1 x0 x1 A0 A1 x2 x3 e0+ e1+ A2 A3 C3 C2 C1 C0 A4 A5 r3+ A6 C5 C4 Z7 Z6 A7"
-S_STEADY = "A0 A1 e0+ e1+ A2 C3 C2 C1 C0 A3 A4 A5 C5 C4 A6 Z7 Z6 A7"
-PE_LAST = "c0 a0 b2 b3 c1 a1 c2 c3 b4 b5 a2 b6 b7 c4 c5 c6 c7 a3 a4 a5 a6 a7"
-V_LAST = "D1 s1 s0 s3 s2 s5 s4 s7 s6"
-S_LAST = "A0 A1 C3 C2 C1 C0 A2 C7 C6 C5 C4 A3 A4 A5"
+PE_FIRST = "T0 T1 X0 Y0 b0 b1 X1 b2 Y1 c0 c1 b3 a0 a1 X2 X3 T0+ T1+ b4 b5 c2 c3 a2 a3 c4 a4 b6 Y2 Y3 c5 a5 b7 c6 a6 b0+ b1+ a7"
+PE_STEADY = "b2 b3 c0 c1 a0 b4 b5 a1 T0+ T1+ c2 c3 a2 a3 b6 b7 c4 c5 c6 a4 a5 b0+ b1+ a6 a7"
+V_FIRST = "r0 W d0 r1 s0 d1 s1 r2 s2 s3 D1 r0p+ s5 s4 W+ r2+ D0+ xs s7 s6"
+V_STEADY = "D1 s1 s0 s3 s2 s5 s4 r0+ W+ D0+ s7 s6"
+S_FIRST = "e0 e1 x0 x1 r3 A0 A1 x2 x3 e0+ e1+ A2 A3 C3 C2 C1 C0 A4 A5 r3+ A6 C6 C5 C4 Z7 A7"
+S_STEADY = "A0 A1 e0+ e1+ A2 C3 C2 C1 C0 A3 A4 A5 A6 C6 C5 C4 Z7 A7"
+PE_LAST = "b2 b3 c0 c1 c2 c3 b4 b5 a0 c4 c5 c6 c7 b6 b7 a1 a2 a3 a4 a5 a6 a7"
+V_LAST = "D1 s1 s0 s3 s2 s5 s4 s7 R s6"
+S_LAST = "C3 C2 C1 C0 A0 C7 C6 C5 C4 A1 A2 A3 A4 A5"
 G_LAST = ""
 S_TAIL = "A6 A7"
 G_FIRST = ""
-G_STEADY = "r2+ r3+"
+G_STEADY = "r2+ r3+ r1+"
 
 
 def tile_cssrclassifier_pa_kernel(tc, d, W_dec, x, out_0, out_1, out_2):
@@ -52,7 +52,6 @@ def tile_cssrclassifier_pa_kernel(tc, d, W_dec, x, out_0, out_1, out_2):
 
         smax = const.tile([P, 64], F32)
         sr01 = const.tile([P, 64], F32)
-        sx = const.tile([P, 8], F32)
         sx01 = const.tile([P, 8], F32)
         x_sb = const.tile([P, NB, 4, NW], BF16)
         x_t = const.tile([P, 8, NC], BF16)
@@ -81,8 +80,8 @@ def tile_cssrclassifier_pa_kernel(tc, d, W_dec, x, out_0, out_1, out_2):
                 in_=x[b0:b1].rearrange("b (p t) h w -> p b (t h w)", t=4),
             )
 
-        load_w(0, 0, 2)
-        load_w(0, 2, 4)
+        for t in range(4):
+            load_w(0, t, t + 1)
         load_d(0, 0, 1)
         load_x(0, 1)
         load_d(0, 1, 2)
@@ -101,6 +100,8 @@ def tile_cssrclassifier_pa_kernel(tc, d, W_dec, x, out_0, out_1, out_2):
         make_identity(nc, ident_f[:])
         ident_b = const.tile([P, P], BF16)
         make_identity(nc, ident_b[:])
+        ones_b = const.tile([P, 1], BF16)
+        nc.vector.memset(ones_b[:], 1.0)
         warm = const.tile([P, 1], F32)
         nc.vector.memset(warm[:], 0.0)
         warm2 = const.tile([P, 1], F32)
@@ -119,7 +120,7 @@ def tile_cssrclassifier_pa_kernel(tc, d, W_dec, x, out_0, out_1, out_2):
             state[("wt", k, g)] = wt
 
         def w_exit(k, g, eng="s"):
-            if g == 0:
+            if ("wg", k) not in state:
                 wg_new = grp.tile([P, NC, 4], BF16, name="wg%d" % k, tag="wg", align_bytes=64)
                 state[("wg", k)] = wg_new
             wgf = state[("wg", k)][:].bitcast(F32)
@@ -193,20 +194,28 @@ def tile_cssrclassifier_pa_kernel(tc, d, W_dec, x, out_0, out_1, out_2):
             state[("xp", b)] = xp
 
         def x_exit(b):
-            xp = state[("xp", b)]
+            nc.scalar.copy(out=x_t[:, 2 * b : 2 * b + 2, :], in_=state[("xp", b)][:])
+
+        def x_sum(b):
+            if b == 0:
+                state["sxp"] = psum.tile([P, 8], F32, name="sxp", tag="bank")
             for h in range(2):
-                i = 2 * b + h
-                nc.scalar.activation(out=x_t[:, i, :], in_=xp[:, h, :], func=ACT.Copy, accum_out=sx[:, i : i + 1])
+                for t in range(4):
+                    nc.tensor.matmul(
+                        out=state["sxp"][:, 2 * b + h : 2 * b + h + 1],
+                        lhsT=x_sb[:, b, t, h * P : (h + 1) * P],
+                        rhs=ones_b[:],
+                        start=(t == 0),
+                        stop=(t == 3),
+                    )
 
         def x_scale():
-            nc.vector.tensor_scalar_mul(out=sx01[:], in0=sx[:], scalar1=0.1)
-            if ABS:
-                i0 = ABS[0]
-                n = len(ABS)
-                dst = sr01[:, i0 // 2 * 16 : i0 // 2 * 16 + 2 * (NK - 1)].rearrange("p (k h) -> p h k", h=2)
+            nc.vector.tensor_scalar_mul(out=sx01[:], in0=state["sxp"][:], scalar1=0.1)
+            for i in ABS:
+                c0 = col_of(0, i)
                 nc.vector.tensor_scalar_mul(
-                    out=dst[:, 2 - n : 2],
-                    in0=sx01[:, i0 : i0 + n].unsqueeze(2).to_broadcast([P, n, NK - 1]),
+                    out=sr01[:, c0 : c0 + 2 * (NK - 1) : 2],
+                    in0=sx01[:, i : i + 1].to_broadcast([P, NK - 1]),
                     scalar1=-1.0,
                 )
 
@@ -235,7 +244,7 @@ def tile_cssrclassifier_pa_kernel(tc, d, W_dec, x, out_0, out_1, out_2):
 
         def copy_a(k, i, eng):
             bp, t = divmod(i, 4)
-            n = 2 if k == NK - 1 and bp == 1 else 4
+            n = 2 if k == NK - 1 else 4
             key = ("rec", k, bp, t // n)
             if key not in state:
                 rec_new = recp.tile([P, 2, n, NW], F32, name="rec%d_%d_%d" % (k, bp, t // n), tag="rec")
@@ -254,7 +263,7 @@ def tile_cssrclassifier_pa_kernel(tc, d, W_dec, x, out_0, out_1, out_2):
                     out=out_2[2 * bp : 2 * bp + 2, k].rearrange("b (p t) h w -> p b t (h w)", t=4)[:, :, t0 : t0 + n],
                     in_=rec[:],
                 )
-                if bp == 0 and k + AHEAD < NK:
+                if bp == 0 and t0 == 0 and k + AHEAD < NK:
                     load_class(k + AHEAD)
 
         def mm_b(k, i):
@@ -326,6 +335,23 @@ def tile_cssrclassifier_pa_kernel(tc, d, W_dec, x, out_0, out_1, out_2):
                 out=jc[:], in_=state[("pc", k, i // 4)][:, i % 4, :], func=ACT.Copy, scale=0.1, accum_out=sr01[:, col : col + 1]
             )
 
+        def v4(ap):
+            return ap.rearrange("p (b k h) -> p b k h", b=NB, k=NK, h=2)
+
+        def bc(ap):
+            return ap.rearrange("p (b h) -> p b h", h=2).unsqueeze(2).to_broadcast([P, NB, NK, 2])
+
+        def by_group(ap):
+            return ap.rearrange("p (b k h) -> p b h k", b=NB, k=NK, h=2)
+
+        def groups(ap):
+            return ap.rearrange("p (b h) -> p b h", h=2)
+
+        srx = const.tile([P, 64], F32)
+
+        def sum_rx():
+            nc.vector.tensor_tensor(out=v4(srx[:]), in0=v4(sr01[:]), in1=bc(sx01[:]), op=ALU.add)
+
         def program(first, steady, last):
             ops = []
             for k in range(NK):
@@ -360,9 +386,11 @@ def tile_cssrclassifier_pa_kernel(tc, d, W_dec, x, out_0, out_1, out_2):
         def ready(eng, op):
             t, k = op
             c = t[0]
-            if (c in "TXba" or t in ("c0", "c4")) and live[0] == BANKS:
+            if (c in "TXba" or t in ("Y0", "c0", "c4")) and live[0] == BANKS:
                 return False
             if c in "TX":
+                return True
+            if c == "Y":
                 return True
             if c in "bc":
                 return quantised(k, int(t[1]))
@@ -371,8 +399,10 @@ def tile_cssrclassifier_pa_kernel(tc, d, W_dec, x, out_0, out_1, out_2):
                 return ("W", k) in done and (
                     (("d0", k) in done and ("d1", k) in done) if k == 0 and i < 4 else ("D%d" % (i // 4), k) in done
                 )
+            if t == "R":
+                return all([("C%d" % j, NK - 1) in done for j in range(8)]) and ("xs", 0) in done
             if t == "xs":
-                return ("x3", 0) in done
+                return ("Y3", 0) in done
             if c == "s":
                 return ("b" + t[1], k) in done and ("x%d" % (int(t[1]) // 2), 0) in done
             if c == "C":
@@ -400,11 +430,13 @@ def tile_cssrclassifier_pa_kernel(tc, d, W_dec, x, out_0, out_1, out_2):
         def emit(eng, op):
             t, k = op
             c = t[0]
-            n = 0 if t in ("W", "xs") else int(t[1])
+            n = 0 if t in ("W", "xs", "R") else int(t[1])
             if c == "T":
                 w_t(k, n)
             elif c == "X":
                 x_tr(n)
+            elif c == "Y":
+                x_sum(n)
             elif c == "b":
                 mm_b(k, n)
             elif c == "c":
@@ -413,6 +445,8 @@ def tile_cssrclassifier_pa_kernel(tc, d, W_dec, x, out_0, out_1, out_2):
                 mm_a(k, n)
             elif t == "xs":
                 x_scale()
+            elif t == "R":
+                sum_rx()
             elif c == "s":
                 if direct(k, n):
                     diff(k, n)
@@ -440,9 +474,9 @@ def tile_cssrclassifier_pa_kernel(tc, d, W_dec, x, out_0, out_1, out_2):
                 if t[2:3] == "p":
                     done.add(("r%d" % n, k))
                     done.add(("r%d" % (n + 1), k))
-            if c in "TXba" or t in ("c0", "c4"):
+            if c in "TXba" or t in ("Y0", "c0", "c4"):
                 live[0] += 1
-            elif c in "esA" or t in ("C0", "C4") or (c == "x" and t != "xs"):
+            elif c in "esA" or t in ("C0", "C4", "xs") or (c == "x" and t != "xs"):
                 live[0] -= 1
             done.add((t, k))
 
@@ -456,20 +490,6 @@ def tile_cssrclassifier_pa_kernel(tc, d, W_dec, x, out_0, out_1, out_2):
                     moved = True
             assert moved, str({e: p[:2] for e, p in left.items()})
 
-        def v4(ap):
-            return ap.rearrange("p (b k h) -> p b k h", b=NB, k=NK, h=2)
-
-        def bc(ap):
-            return ap.rearrange("p (b h) -> p b h", h=2).unsqueeze(2).to_broadcast([P, NB, NK, 2])
-
-        def by_group(ap):
-            return ap.rearrange("p (b k h) -> p b h k", b=NB, k=NK, h=2)
-
-        def groups(ap):
-            return ap.rearrange("p (b h) -> p b h", h=2)
-
-        srx = const.tile([P, 64], F32)
-        nc.vector.tensor_tensor(out=v4(srx[:]), in0=v4(sr01[:]), in1=bc(sx01[:]), op=ALU.add)
         t1 = const.tile([P, 64], F32)
         nc.vector.scalar_tensor_tensor(out=t1[:], in0=smax[:], scalar=-0.2, in1=srx[:], op0=ALU.mult, op1=ALU.add)
         lg = const.tile([P, 64], F32)
@@ -503,7 +523,7 @@ def tile_cssrclassifier_pa_kernel(tc, d, W_dec, x, out_0, out_1, out_2):
         )
         e_out = const.tile([P, NK], F32)
         nc.vector.tensor_reduce(out=e_out[:], in_=e_sel[:].rearrange("p b k -> p k b"), axis=AX.X, op=ALU.add)
-        nc.sync.dma_start(out=out_1, in_=e_out[0:NB, :])
+        nc.scalar.dma_start(out=out_1, in_=e_out[0:NB, :])
         p_out = const.tile([P, P], F32)
         nc.vector.tensor_copy(out=p_out[:], in_=pt[:])
-        nc.sync.dma_start(out=out_0.rearrange("b k (h r) w -> (b k h) (r w)", h=2), in_=p_out[0:64, :])
+        nc.scalar.dma_start(out=out_0.rearrange("b k (h r) w -> (b k h) (r w)", h=2), in_=p_out[0:64, :])

@@ -18,21 +18,23 @@ FLOPS = 2 * NK * NB * NC * NJ * NW
 
 GRP = 2
 GRP1 = 1
-ABS = (7,)
+ABS = (5, 6, 7)
 AHEAD = 4
 MANUAL = True
+LOADS = "w01 w12 w23 w34 d01 x01 d12 x12 d24 x24"
 BANKS = 8
-PE_FIRST = "T0 T1 X0 Y0 b0 b1 X1 b2 Y1 c0 c1 b3 a0 a1 X2 X3 T0+ T1+ b4 b5 c2 c3 a2 a3 c4 a4 b6 Y2 Y3 c5 a5 b7 c6 a6 b0+ b1+ a7"
-PE_STEADY = "b2 b3 c0 c1 a0 b4 b5 a1 T0+ T1+ c2 c3 a2 a3 b6 b7 c4 c5 c6 a4 a5 b0+ b1+ a6 a7"
+PE_FIRST = "T0 T1 X0 Y0 b0 b1 X1 b2 Y1 c0 c1 b3 a0 a1 X2 X3 T0+ T1+ b4 b5 c2 c3 a2 a3 c4 a4 b6 Y2 Y3 a5 b7 a6 b0+ b1+ a7"
+PE_STEADY = "b2 b3 c0 c1 a0 b4 b5 a1 T0+ T1+ c2 c3 a2 a3 b6 b7 c4 a4 a5 b0+ b1+ a6 a7"
 V_FIRST = "r0 W d0 r1 s0 d1 s1 r2 s2 s3 D1 r0p+ s5 s4 W+ r2+ D0+ xs s7 s6"
-V_STEADY = "D1 s1 s0 s3 s2 s5 s4 r0+ W+ D0+ s7 s6"
-S_FIRST = "e0 e1 x0 x1 r3 A0 A1 x2 x3 e0+ e1+ A2 A3 C3 C2 C1 C0 A4 A5 r3+ A6 C6 C5 C4 Z7 A7"
-S_STEADY = "A0 A1 e0+ e1+ A2 C3 C2 C1 C0 A3 A4 A5 A6 C6 C5 C4 Z7 A7"
+V_STEADY = "D1 s1 s0 s3 s2 s5 s4 e1+ r0+ W+ D0+ s7 s6"
+S_FIRST = "e0 e1 x0 x1 r3 A0 A1 x2 x3 e0+ e1+ A2 A3 C3 C2 C1 C0 A4 Z5 A5 r3+ A6 C4 Z7 Z6 A7"
+S_STEADY = "A0 A1 e0+ A2 C3 C2 C1 C0 A3 A4 Z5 A5 A6 C4 Z7 Z6 A7"
 PE_LAST = "b2 b3 c0 c1 c2 c3 b4 b5 a0 c4 c5 c6 c7 b6 b7 a1 a2 a3 a4 a5 a6 a7"
 V_LAST = "D1 s1 s0 s3 s2 s5 s4 s7 R s6"
-S_LAST = "C3 C2 C1 C0 A0 C7 C6 C5 C4 A1 A2 A3 A4 A5"
+S_LAST = "C3 C2 C1 C0 A0 C7 C6 C5 C4 A1 A2 A3"
 G_LAST = ""
-S_TAIL = "A6 A7"
+S_TAIL = "A4 A5 A6 A7"
+V_TAIL = ""
 G_FIRST = ""
 G_STEADY = "r2+ r3+ r1+"
 
@@ -80,14 +82,9 @@ def tile_cssrclassifier_pa_kernel(tc, d, W_dec, x, out_0, out_1, out_2):
                 in_=x[b0:b1].rearrange("b (p t) h w -> p b (t h w)", t=4),
             )
 
-        for t in range(4):
-            load_w(0, t, t + 1)
-        load_d(0, 0, 1)
-        load_x(0, 1)
-        load_d(0, 1, 2)
-        load_x(1, 2)
-        load_d(0, 2, 4)
-        load_x(2, 4)
+        for tok in LOADS.split(" "):
+            lo, hi = int(tok[1]), int(tok[2])
+            {"w": lambda lo, hi: load_w(0, lo, hi), "d": lambda lo, hi: load_d(0, lo, hi), "x": load_x}[tok[0]](lo, hi)
         def load_class(k):
             load_w(k)
             load_d(k, 0, 2)
@@ -244,7 +241,7 @@ def tile_cssrclassifier_pa_kernel(tc, d, W_dec, x, out_0, out_1, out_2):
 
         def copy_a(k, i, eng):
             bp, t = divmod(i, 4)
-            n = 2 if k == NK - 1 else 4
+            n = (2 - bp) if k == NK - 1 else 4
             key = ("rec", k, bp, t // n)
             if key not in state:
                 rec_new = recp.tile([P, 2, n, NW], F32, name="rec%d_%d_%d" % (k, bp, t // n), tag="rec")
@@ -336,13 +333,13 @@ def tile_cssrclassifier_pa_kernel(tc, d, W_dec, x, out_0, out_1, out_2):
             )
 
         def v4(ap):
-            return ap.rearrange("p (b k h) -> p b k h", b=NB, k=NK, h=2)
+            return ap.rearrange("p (b k h) -> p b k h", k=NK, h=2)
 
         def bc(ap):
-            return ap.rearrange("p (b h) -> p b h", h=2).unsqueeze(2).to_broadcast([P, NB, NK, 2])
+            return ap.rearrange("p (b h) -> p b h", h=2).unsqueeze(2).to_broadcast([P, ap.shape[1] // 2, NK, 2])
 
         def by_group(ap):
-            return ap.rearrange("p (b k h) -> p b h k", b=NB, k=NK, h=2)
+            return ap.rearrange("p (b k h) -> p b h k", k=NK, h=2)
 
         def groups(ap):
             return ap.rearrange("p (b h) -> p b h", h=2)
@@ -490,28 +487,42 @@ def tile_cssrclassifier_pa_kernel(tc, d, W_dec, x, out_0, out_1, out_2):
                     moved = True
             assert moved, str({e: p[:2] for e, p in left.items()})
 
+        halves = [(slice(0, 32), slice(0, 4)), (slice(32, 64), slice(4, 8))]
         t1 = const.tile([P, 64], F32)
-        nc.vector.scalar_tensor_tensor(out=t1[:], in0=smax[:], scalar=-0.2, in1=srx[:], op0=ALU.mult, op1=ALU.add)
         lg = const.tile([P, 64], F32)
-        nc.vector.tensor_scalar(out=lg[:], in0=t1[:], scalar1=-500.0, scalar2=500.0, op0=ALU.max, op1=ALU.min)
         mxk = const.tile([P, 8], F32)
-        nc.vector.tensor_reduce(out=groups(mxk[:]), in_=by_group(lg[:]), axis=AX.X, op=ALU.max)
         sh = const.tile([P, 64], F32)
-        nc.vector.tensor_tensor(out=v4(sh[:]), in0=v4(lg[:]), in1=bc(mxk[:]), op=ALU.subtract)
         ex = const.tile([P, 64], F32)
-        nc.scalar.activation(out=ex[:], in_=sh[:], func=ACT.Exp)
+        den = const.tile([P, 8], F32)
+        rden = const.tile([P, 8], F32)
+        lsum = const.tile([P, 32], F32)
+        for c, g in halves:
+            nc.vector.scalar_tensor_tensor(
+                out=t1[:, c], in0=smax[:, c], scalar=-0.2, in1=srx[:, c], op0=ALU.mult, op1=ALU.add
+            )
+        for c, g in halves:
+            nc.vector.tensor_scalar(out=lg[:, c], in0=t1[:, c], scalar1=-500.0, scalar2=500.0, op0=ALU.max, op1=ALU.min)
+        for c, g in halves:
+            nc.vector.tensor_reduce(out=groups(mxk[:, g]), in_=by_group(lg[:, c]), axis=AX.X, op=ALU.max)
+        for c, g in halves:
+            nc.vector.tensor_tensor(out=v4(sh[:, c]), in0=v4(lg[:, c]), in1=bc(mxk[:, g]), op=ALU.subtract)
+        for c, g in halves:
+            nc.scalar.activation(out=ex[:, c], in_=sh[:, c], func=ACT.Exp)
         for tok in S_TAIL.split(" "):
             emit("S", (tok, NK - 1))
-        lsum = const.tile([P, 32], F32)
         lg3 = lg[:].rearrange("p (c h) -> p c h", h=2)
         nc.vector.tensor_tensor(out=lsum[:], in0=lg3[:, :, 0], in1=lg3[:, :, 1], op=ALU.add)
+        for tok in V_TAIL.split(" "):
+            if tok:
+                emit("V", (tok, NK - 1))
         pmean = psum.tile([P, 32], F32, name="pmean", tag="bank")
         nc.tensor.matmul(out=pmean[:], lhsT=ones_f[:], rhs=lsum[:], start=True, stop=True)
-        den = const.tile([P, 8], F32)
-        nc.vector.tensor_reduce(out=groups(den[:]), in_=by_group(ex[:]), axis=AX.X, op=ALU.add)
-        rden = const.tile([P, 8], F32)
-        nc.vector.reciprocal(out=rden[:], in_=den[:])
-        nc.vector.tensor_tensor(out=v4(pad[:, 0:64]), in0=v4(ex[:]), in1=bc(rden[:]), op=ALU.mult)
+        for c, g in halves:
+            nc.vector.tensor_reduce(out=groups(den[:, g]), in_=by_group(ex[:, c]), axis=AX.X, op=ALU.add)
+        for c, g in halves:
+            nc.vector.reciprocal(out=rden[:, g], in_=den[:, g])
+        for c, g in halves:
+            nc.vector.tensor_tensor(out=v4(pad[:, c]), in0=v4(ex[:, c]), in1=bc(rden[:, g]), op=ALU.mult)
         pt = psum.tile([P, P], F32, name="pt", tag="bank")
         nc.tensor.transpose(pt[:], pad[:], ident_f[:])
         e_sel = const.tile([P, NB, NK], F32)

@@ -23,20 +23,22 @@ AHEAD = 4
 MANUAL = True
 LOADS = "w01 w12 w23 w34 d01 x01 d12 x12 d24 x24"
 BANKS = 8
+FINE = ((4, 4), (4, 4), (4, 4), (4, 4), (4, 4), (4, 4), (4, 4), (2, 1))
 PE_FIRST = "T0 T1 X0 Y0 b0 b1 X1 b2 Y1 c0 c1 b3 a0 a1 X2 X3 T0+ T1+ b4 b5 c2 c3 a2 a3 c4 a4 b6 Y2 Y3 a5 b7 a6 b0+ b1+ a7"
 PE_STEADY = "b2 b3 c0 c1 a0 b4 b5 a1 T0+ T1+ c2 c3 a2 a3 b6 b7 c4 a4 a5 b0+ b1+ a6 a7"
 V_FIRST = "r0 W d0 r1 s0 d1 s1 r2 s2 s3 D1 r0p+ s5 s4 W+ r2+ D0+ xs s7 s6"
-V_STEADY = "D1 s1 s0 s3 s2 s5 s4 e1+ r0+ W+ D0+ s7 s6"
+V_STEADY = "D1 s1 s0 s3 s2 s5 s4 r0p+ W+ D0+ s7 s6"
 S_FIRST = "e0 e1 x0 x1 r3 A0 A1 x2 x3 e0+ e1+ A2 A3 C3 C2 C1 C0 A4 Z5 A5 r3+ A6 C4 Z7 Z6 A7"
-S_STEADY = "A0 A1 e0+ A2 C3 C2 C1 C0 A3 A4 Z5 A5 A6 C4 Z7 Z6 A7"
-PE_LAST = "b2 b3 c0 c1 c2 c3 b4 b5 a0 c4 c5 c6 c7 b6 b7 a1 a2 a3 a4 a5 a6 a7"
-V_LAST = "D1 s1 s0 s3 s2 s5 s4 s7 R s6"
-S_LAST = "C3 C2 C1 C0 A0 C7 C6 C5 C4 A1 A2 A3"
+S_STEADY = "A0 A1 e0+ e1+ A2 C3 C2 C1 C0 A3 A4 Z5 A5 A6 C4 Z7 Z6 A7"
+PE_LAST = "b2 b3 a0 c0 c1 c2 c3 b4 b5 a1 c4 c5 c6 c7 b6 b7 a2 a3 a4 a5 a6 a7"
+V_LAST = "D1 s1 s0 s3 s2 A0 s5 s4 A1 s7 R s6"
+S_LAST = "C3 C2 C1 C0 C7 C6 C5 C4 A2 A3 A4 A5"
 G_LAST = ""
-S_TAIL = "A4 A5 A6 A7"
+S_TAIL = "A6 A7"
 V_TAIL = ""
+S_TAIL2 = ""
 G_FIRST = ""
-G_STEADY = "r2+ r3+ r1+"
+G_STEADY = "r2+ r3+"
 
 
 def tile_cssrclassifier_pa_kernel(tc, d, W_dec, x, out_0, out_1, out_2):
@@ -241,7 +243,7 @@ def tile_cssrclassifier_pa_kernel(tc, d, W_dec, x, out_0, out_1, out_2):
 
         def copy_a(k, i, eng):
             bp, t = divmod(i, 4)
-            n = (2 - bp) if k == NK - 1 else 4
+            n = FINE[k][bp]
             key = ("rec", k, bp, t // n)
             if key not in state:
                 rec_new = recp.tile([P, 2, n, NW], F32, name="rec%d_%d_%d" % (k, bp, t // n), tag="rec")
@@ -509,7 +511,8 @@ def tile_cssrclassifier_pa_kernel(tc, d, W_dec, x, out_0, out_1, out_2):
         for c, g in halves:
             nc.scalar.activation(out=ex[:, c], in_=sh[:, c], func=ACT.Exp)
         for tok in S_TAIL.split(" "):
-            emit("S", (tok, NK - 1))
+            if tok:
+                emit("S", (tok, NK - 1))
         lg3 = lg[:].rearrange("p (c h) -> p c h", h=2)
         nc.vector.tensor_tensor(out=lsum[:], in0=lg3[:, :, 0], in1=lg3[:, :, 1], op=ALU.add)
         for tok in V_TAIL.split(" "):
@@ -538,3 +541,6 @@ def tile_cssrclassifier_pa_kernel(tc, d, W_dec, x, out_0, out_1, out_2):
         p_out = const.tile([P, P], F32)
         nc.vector.tensor_copy(out=p_out[:], in_=pt[:])
         nc.scalar.dma_start(out=out_0.rearrange("b k (h r) w -> (b k h) (r w)", h=2), in_=p_out[0:64, :])
+        for tok in S_TAIL2.split(" "):
+            if tok:
+                emit("S", (tok, NK - 1))

@@ -18,18 +18,18 @@ FLOPS = 2 * NK * NB * NC * NJ * NW
 
 GRP = 2
 GRP1 = 1
-ABS = (5, 6, 7)
+ABS = (6, 7)
 AHEAD = 4
 MANUAL = True
 LOADS = "w01 w12 w23 w34 d01 x01 d12 x12 d24 x24"
 BANKS = 8
 FINE = ((4, 4), (4, 4), (4, 4), (4, 4), (4, 4), (4, 4), (4, 4), (2, 1))
-PE_FIRST = "T0 T1 X0 Y0 b0 b1 X1 b2 Y1 c0 c1 b3 a0 a1 X2 X3 T0+ T1+ b4 b5 c2 c3 a2 a3 c4 a4 b6 Y2 Y3 a5 b7 a6 b0+ b1+ a7"
-PE_STEADY = "b2 b3 c0 c1 a0 b4 b5 a1 T0+ T1+ c2 c3 a2 a3 b6 b7 c4 a4 a5 b0+ b1+ a6 a7"
+PE_FIRST = "T0 T1 X0 Y0 b0 b1 X1 b2 Y1 c0 c1 b3 a0 a1 X2 X3 T0+ T1+ b4 b5 c2 c3 a2 a3 c4 a4 b6 Y2 Y3 c5 a5 b7 a6 b0+ b1+ a7"
+PE_STEADY = "b2 b3 c0 c1 a0 b4 b5 a1 T0+ T1+ c2 c3 a2 a3 b6 b7 c4 c5 a4 a5 b0+ b1+ a6 a7"
 V_FIRST = "r0 W d0 r1 s0 d1 s1 r2 s2 s3 D1 r0p+ s5 s4 W+ r2+ D0+ xs s7 s6"
 V_STEADY = "D1 s1 s0 s3 s2 s5 s4 r0p+ W+ D0+ s7 s6"
-S_FIRST = "e0 e1 x0 x1 r3 A0 A1 x2 x3 e0+ e1+ A2 A3 C3 C2 C1 C0 A4 Z5 A5 r3+ A6 C4 Z7 Z6 A7"
-S_STEADY = "A0 A1 e0+ e1+ A2 C3 C2 C1 C0 A3 A4 Z5 A5 A6 C4 Z7 Z6 A7"
+S_FIRST = "e0 e1 x0 x1 r3 A0 A1 x2 x3 e0+ e1+ A2 A3 C3 C2 C1 C0 A4 A5 r3+ A6 C5 C4 Z7 Z6 A7"
+S_STEADY = "A0 A1 e0+ e1+ A2 C3 C2 C1 C0 A3 A4 A5 A6 C5 C4 Z7 Z6 A7"
 PE_LAST = "b2 b3 a0 c0 c1 c2 c3 b4 b5 a1 c4 c5 c6 c7 b6 b7 a2 a3 a4 a5 a6 a7"
 V_LAST = "D1 s1 s0 s3 s2 A0 s5 s4 A1 s7 R s6"
 S_LAST = "C3 C2 C1 C0 C7 C6 C5 C4 A2 A3 A4 A5"

@@ -24,20 +24,24 @@ MANUAL = True
 LOADS = "w01 w12 w23 w34 d01 x01 d12 x12 d24 x24"
 BANKS = 8
 FINE = ((4, 4), (4, 4), (4, 4), (4, 4), (4, 4), (4, 4), (4, 4), (2, 1))
-PE_FIRST = "T0 T1 X0 Y0 b0 b1 X1 b2 Y1 c0 c1 b3 a0 a1 X2 X3 T0+ T1+ b4 b5 c2 c3 a2 a3 c4 a4 b6 Y2 Y3 c5 a5 b7 a6 b0+ b1+ a7"
+PE_FIRST = "K0 K0 K0 K0 K0 T0 T1 K0 K0 X0 Y0 K0 K0 b0 b1 X1 b2 Y1 c0 c1 b3 a0 a1 X2 X3 T0+ T1+ b4 b5 c2 c3 a2 a3 c4 a4 b6 Y2 Y3 c5 a5 b7 a6 b0+ b1+ a7"
 PE_STEADY = "b2 b3 c0 c1 a0 b4 b5 a1 T0+ T1+ c2 c3 a2 a3 b6 b7 c4 c5 a4 a5 b0+ b1+ a6 a7"
 V_FIRST = "r0 W d0 r1 s0 d1 s1 r2 s2 s3 D1 r0p+ s5 s4 W+ r2+ D0+ xs s7 s6"
 V_STEADY = "D1 s1 s0 s3 s2 s5 s4 r0p+ W+ D0+ s7 s6"
-S_FIRST = "e0 e1 x0 x1 r3 A0 A1 x2 x3 e0+ e1+ A2 A3 C3 C2 C1 C0 A4 A5 r3+ A6 C5 C4 Z7 Z6 A7"
+S_FIRST = "e0 e1 x0 x1 r3 A0 A1 x2 x3 e0+ e1+ A2 A3 C3 C2 C1 C0 A4 A5 A6 C5 C4 Z7 Z6 A7"
 S_STEADY = "A0 A1 e0+ e1+ A2 C3 C2 C1 C0 A3 A4 A5 A6 C5 C4 Z7 Z6 A7"
 PE_LAST = "b2 b3 a0 c0 c1 c2 c3 b4 b5 a1 c4 c5 c6 c7 b6 b7 a2 a3 a4 a5 a6 a7"
 V_LAST = "D1 s1 s0 s3 s2 A0 s5 s4 A1 s7 R s6"
 S_LAST = "C3 C2 C1 C0 C7 C6 C5 C4 A2 A3 A4 A5"
+PE_ODD = ""
+V_ODD = ""
+S_ODD = ""
+G_ODD = ""
 G_LAST = ""
 S_TAIL = "A6 A7"
 V_TAIL = ""
 S_TAIL2 = ""
-G_FIRST = ""
+G_FIRST = "r3+"
 G_STEADY = "r2+ r3+"
 
 
@@ -55,8 +59,8 @@ def tile_cssrclassifier_pa_kernel(tc, d, W_dec, x, out_0, out_1, out_2):
             ctx.enter_context(tc.manual_schedule())
 
         smax = const.tile([P, 64], F32)
-        sr01 = const.tile([P, 64], F32)
-        sx01 = const.tile([P, 8], F32)
+        sr = const.tile([P, 64], F32)
+        sx = const.tile([P, 8], F32)
         x_sb = const.tile([P, NB, 4, NW], BF16)
         x_t = const.tile([P, 8, NC], BF16)
         state = {}
@@ -95,6 +99,8 @@ def tile_cssrclassifier_pa_kernel(tc, d, W_dec, x, out_0, out_1, out_2):
         for k in range(1, AHEAD):
             load_class(k)
 
+        zeros_b = const.tile([P, NW], BF16)
+        nc.vector.memset(zeros_b[:], 0.0)
         ident_f = const.tile([P, P], F32)
         make_identity(nc, ident_f[:])
         ident_b = const.tile([P, P], BF16)
@@ -185,6 +191,11 @@ def tile_cssrclassifier_pa_kernel(tc, d, W_dec, x, out_0, out_1, out_2):
         def q_d(k, bp):
             q_d_cols(k, 2 * bp, 2 * bp + 2)
 
+        def warm_up():
+            if "warm" not in state:
+                state["warm"] = psum.tile([P, NW], F32, name="warm_out", tag="bank")
+            nc.tensor.matmul(out=state["warm"][:], lhsT=zeros_b[:, 0:P], rhs=zeros_b[:], start=True, stop=True)
+
         def x_tr(b):
             xp = psum.tile([P, 2, NC], BF16, name="xp%d" % b, tag="bank")
             for h in range(2):
@@ -209,12 +220,12 @@ def tile_cssrclassifier_pa_kernel(tc, d, W_dec, x, out_0, out_1, out_2):
                     )
 
         def x_scale():
-            nc.vector.tensor_scalar_mul(out=sx01[:], in0=state["sxp"][:], scalar1=0.1)
+            nc.vector.tensor_copy(out=sx[:], in_=state["sxp"][:])
             for i in ABS:
                 c0 = col_of(0, i)
                 nc.vector.tensor_scalar_mul(
-                    out=sr01[:, c0 : c0 + 2 * (NK - 1) : 2],
-                    in0=sx01[:, i : i + 1].to_broadcast([P, NK - 1]),
+                    out=sr[:, c0 : c0 + 2 * (NK - 1) : 2],
+                    in0=sx[:, i : i + 1].to_broadcast([P, NK - 1]),
                     scalar1=-1.0,
                 )
 
@@ -327,11 +338,17 @@ def tile_cssrclassifier_pa_kernel(tc, d, W_dec, x, out_0, out_1, out_2):
                 out=ja[:], in_=state[("df", k, i)][:], func=ACT.Abs, scale=0.5, accum_out=smax[:, col : col + 1]
             )
 
+        def creduce(k, g):
+            dst = sr[:, g * 32 : g * 32 + 32].rearrange("p (b k h) -> p b k h", b=2, k=NK)[:, :, k, :]
+            nc.vector.tensor_reduce(
+                out=dst, in_=state[("pc", k, g)][:].rearrange("p (b h) c -> p b h c", b=2), axis=AX.X, op=ALU.add
+            )
+
         def cacc(k, i):
             col = col_of(k, i)
             jc = junk.tile([P, P], BF16, name="jc%d_%d" % (k, i), tag="jc")
             nc.scalar.activation(
-                out=jc[:], in_=state[("pc", k, i // 4)][:, i % 4, :], func=ACT.Copy, scale=0.1, accum_out=sr01[:, col : col + 1]
+                out=jc[:], in_=state[("pc", k, i // 4)][:, i % 4, :], func=ACT.Copy, accum_out=sr[:, col : col + 1]
             )
 
         def v4(ap):
@@ -349,12 +366,12 @@ def tile_cssrclassifier_pa_kernel(tc, d, W_dec, x, out_0, out_1, out_2):
         srx = const.tile([P, 64], F32)
 
         def sum_rx():
-            nc.vector.tensor_tensor(out=v4(srx[:]), in0=v4(sr01[:]), in1=bc(sx01[:]), op=ALU.add)
+            nc.vector.tensor_tensor(out=v4(srx[:]), in0=v4(sr[:]), in1=bc(sx[:]), op=ALU.add)
 
-        def program(first, steady, last):
+        def program(first, steady, odd, last):
             ops = []
             for k in range(NK):
-                for tok in (first if k == 0 else last if k == NK - 1 else steady).split(" "):
+                for tok in (first if k == 0 else last if k == NK - 1 else odd if k % 2 and odd else steady).split(" "):
                     if tok == "":
                         continue
                     kk = k + (1 if "+" in tok else 0)
@@ -363,10 +380,10 @@ def tile_cssrclassifier_pa_kernel(tc, d, W_dec, x, out_0, out_1, out_2):
             return ops
 
         progs = {
-            "PE": program(PE_FIRST, PE_STEADY, PE_LAST),
-            "V": program(V_FIRST, V_STEADY, V_LAST),
-            "S": program(S_FIRST, S_STEADY, S_LAST),
-            "G": program(G_FIRST, G_STEADY, G_LAST),
+            "PE": program(PE_FIRST, PE_STEADY, PE_ODD, PE_LAST),
+            "V": program(V_FIRST, V_STEADY, V_ODD, V_LAST),
+            "S": program(S_FIRST, S_STEADY, S_ODD, S_LAST),
+            "G": program(G_FIRST, G_STEADY, G_ODD, G_LAST),
         }
         order = {}
         done = set()
@@ -389,7 +406,7 @@ def tile_cssrclassifier_pa_kernel(tc, d, W_dec, x, out_0, out_1, out_2):
                 return False
             if c in "TX":
                 return True
-            if c == "Y":
+            if c in "YK":
                 return True
             if c in "bc":
                 return quantised(k, int(t[1]))
@@ -399,11 +416,13 @@ def tile_cssrclassifier_pa_kernel(tc, d, W_dec, x, out_0, out_1, out_2):
                     (("d0", k) in done and ("d1", k) in done) if k == 0 and i < 4 else ("D%d" % (i // 4), k) in done
                 )
             if t == "R":
-                return all([("C%d" % j, NK - 1) in done for j in range(8)]) and ("xs", 0) in done
+                return all([("C%d" % j, NK - 1) in done or ("M%d" % (j // 4), NK - 1) in done for j in range(8)]) and ("xs", 0) in done
             if t == "xs":
                 return ("Y3", 0) in done
             if c == "s":
                 return ("b" + t[1], k) in done and ("x%d" % (int(t[1]) // 2), 0) in done
+            if c == "M":
+                return all([("c%d" % (4 * int(t[1]) + j), k) in done for j in range(4)])
             if c == "C":
                 return all([("c%d" % j, k) in done for j in range(int(t[1]) // 4 * 4, int(t[1]) // 4 * 4 + 4) if not direct(k, j)])
             if c == "Z":
@@ -434,6 +453,8 @@ def tile_cssrclassifier_pa_kernel(tc, d, W_dec, x, out_0, out_1, out_2):
                 w_t(k, n)
             elif c == "X":
                 x_tr(n)
+            elif c == "K":
+                warm_up()
             elif c == "Y":
                 x_sum(n)
             elif c == "b":
@@ -453,6 +474,8 @@ def tile_cssrclassifier_pa_kernel(tc, d, W_dec, x, out_0, out_1, out_2):
                     stt(k, n)
             elif c == "Z":
                 absacc(k, n)
+            elif c == "M":
+                creduce(k, n)
             elif c == "C":
                 cacc(k, n)
             elif c == "A":
@@ -475,7 +498,7 @@ def tile_cssrclassifier_pa_kernel(tc, d, W_dec, x, out_0, out_1, out_2):
                     done.add(("r%d" % (n + 1), k))
             if c in "TXba" or t in ("Y0", "c0", "c4"):
                 live[0] += 1
-            elif c in "esA" or t in ("C0", "C4", "xs") or (c == "x" and t != "xs"):
+            elif c in "esA" or t in ("C0", "C4", "xs", "M0", "M1") or (c == "x" and t != "xs"):
                 live[0] -= 1
             done.add((t, k))
 
@@ -500,16 +523,16 @@ def tile_cssrclassifier_pa_kernel(tc, d, W_dec, x, out_0, out_1, out_2):
         lsum = const.tile([P, 32], F32)
         for c, g in halves:
             nc.vector.scalar_tensor_tensor(
-                out=t1[:, c], in0=smax[:, c], scalar=-0.2, in1=srx[:, c], op0=ALU.mult, op1=ALU.add
+                out=t1[:, c], in0=smax[:, c], scalar=-2.0, in1=srx[:, c], op0=ALU.mult, op1=ALU.add
             )
         for c, g in halves:
-            nc.vector.tensor_scalar(out=lg[:, c], in0=t1[:, c], scalar1=-500.0, scalar2=500.0, op0=ALU.max, op1=ALU.min)
+            nc.vector.tensor_scalar(out=lg[:, c], in0=t1[:, c], scalar1=-5000.0, scalar2=5000.0, op0=ALU.max, op1=ALU.min)
         for c, g in halves:
             nc.vector.tensor_reduce(out=groups(mxk[:, g]), in_=by_group(lg[:, c]), axis=AX.X, op=ALU.max)
         for c, g in halves:
             nc.vector.tensor_tensor(out=v4(sh[:, c]), in0=v4(lg[:, c]), in1=bc(mxk[:, g]), op=ALU.subtract)
         for c, g in halves:
-            nc.scalar.activation(out=ex[:, c], in_=sh[:, c], func=ACT.Exp)
+            nc.scalar.activation(out=ex[:, c], in_=sh[:, c], func=ACT.Exp, scale=0.1)
         for tok in S_TAIL.split(" "):
             if tok:
                 emit("S", (tok, NK - 1))
@@ -529,11 +552,13 @@ def tile_cssrclassifier_pa_kernel(tc, d, W_dec, x, out_0, out_1, out_2):
         pt = psum.tile([P, P], F32, name="pt", tag="bank")
         nc.tensor.transpose(pt[:], pad[:], ident_f[:])
         e_sel = const.tile([P, NB, NK], F32)
-        nc.vector.tensor_tensor(
+        nc.vector.scalar_tensor_tensor(
             out=e_sel[:],
             in0=pmean[:].rearrange("p (b k) -> p b k", b=NB),
+            scalar=0.1,
             in1=ident_f[:, 0:NB].unsqueeze(2).to_broadcast([P, NB, NK]),
-            op=ALU.mult,
+            op0=ALU.mult,
+            op1=ALU.mult,
         )
         e_out = const.tile([P, NK], F32)
         nc.vector.tensor_reduce(out=e_out[:], in_=e_sel[:].rearrange("p b k -> p k b"), axis=AX.X, op=ALU.add)

from contextlib import ExitStack

import concourse.mybir as mybir
from concourse.masks import make_identity

FP8X4 = mybir.dt.float8_e4m3fn_x4
BF16 = mybir.dt.bfloat16
F32 = mybir.dt.float32
U32 = mybir.dt.uint32
U8 = mybir.dt.uint8
ALU = mybir.AluOpType
ACT = mybir.ActivationFunctionType
AX = mybir.AxisListType

P = 128
NK, NB, NC, NJ, NW = 8, 4, 512, 512, 256
FLOPS = 2 * NK * NB * NC * NJ * NW

GRP = 2
GRP1 = 1
ABS = (6, 7)
AHEAD = 4
MANUAL = True
LOADS = "w01 w12 w23 w34 d01 x01 d12 x12 d24 x24"
BANKS = 8
FINE = ((4, 4), (4, 4), (4, 4), (4, 4), (4, 4), (4, 4), (4, 4), (2, 1))
PE_FIRST = "K0 K0 K0 K0 K0 T0 T1 K0 K0 X0 Y0 K0 K0 b0 b1 X1 b2 Y1 c0 c1 b3 a0 a1 X2 X3 T0+ T1+ b4 b5 c2 c3 a2 a3 c4 a4 b6 Y2 Y3 c5 a5 b7 a6 b0+ b1+ a7"
PE_STEADY = "b2 b3 c0 c1 a0 b4 b5 a1 T0+ T1+ c2 c3 a2 a3 b6 b7 c4 c5 a4 a5 b0+ b1+ a6 a7"
V_FIRST = "r0 W d0 r1 s0 d1 s1 r2 s2 s3 D1 r0p+ s5 s4 W+ r2+ D0+ xs s7 s6"
V_STEADY = "D1 s1 s0 s3 s2 s5 s4 r0p+ W+ D0+ s7 s6"
S_FIRST = "e0 e1 x0 x1 r3 A0 A1 x2 x3 e0+ e1+ A2 A3 C3 C2 C1 C0 A4 A5 A6 C5 C4 Z7 Z6 A7"
S_STEADY = "A0 A1 e0+ e1+ A2 C3 C2 C1 C0 A3 A4 A5 A6 C5 C4 Z7 Z6 A7"
PE_LAST = "b2 b3 a0 c0 c1 c2 c3 b4 b5 a1 c4 c5 c6 c7 b6 b7 a2 a3 a4 a5 a6 a7"
V_LAST = "D1 s1 s0 s3 s2 A0 s5 s4 A1 s7 R s6"
S_LAST = "C3 C2 C1 C0 C7 C6 C5 C4 A2 A3 A4 A5"
PE_ODD = ""
V_ODD = ""
S_ODD = ""
G_ODD = ""
G_LAST = ""
S_TAIL = "A6 A7"
V_TAIL = ""
S_TAIL2 = ""
G_FIRST = "r3+"
G_STEADY = "r2+ r3+"


def tile_cssrclassifier_pa_kernel(tc, d, W_dec, x, out_0, out_1, out_2):
    nc = tc.nc
    with ExitStack() as ctx:
        const = ctx.enter_context(tc.tile_pool(name="const", bufs=1))
        raw = ctx.enter_context(tc.tile_pool(name="raw", bufs=NK))
        grp = ctx.enter_context(tc.tile_pool(name="grp", bufs=GRP))
        mx = ctx.enter_context(tc.tile_pool(name="mx", bufs=3))
        recp = ctx.enter_context(tc.tile_pool(name="recp", bufs=6))
        junk = ctx.enter_context(tc.tile_pool(name="junk", bufs=4))
        psum = ctx.enter_context(tc.psum_pool(name="psum", bufs=BANKS))
        if MANUAL:
            ctx.enter_context(tc.manual_schedule())

        smax = const.tile([P, 64], F32)
        sr = const.tile([P, 64], F32)
        sx = const.tile([P, 8], F32)
        x_sb = const.tile([P, NB, 4, NW], BF16)
        x_t = const.tile([P, 8, NC], BF16)
        state = {}

        def load_w(k, t0=0, t1=4):
            if t0 == 0:
                wr = raw.tile([P, 4, NJ], BF16, name="w_raw%d" % k, tag="w_raw")
                state[("w_raw", k)] = wr
            wr = state[("w_raw", k)]
            nc.sync.dma_start(out=wr[:, t0:t1], in_=W_dec[k].rearrange("(p t) j -> p t j", t=4)[:, t0:t1])

        def load_d(k, b0, b1):
            if b0 == 0:
                dr_new = raw.tile([P, NB, 4, NW], BF16, name="d_raw%d" % k, tag="d_raw")
                state[("d_raw", k)] = dr_new
            dr = state[("d_raw", k)]
            nc.sync.dma_start(
                out=dr[:, b0:b1].rearrange("q b t w -> q b (t w)"),
                in_=d[k, b0:b1].rearrange("b (q t) h w -> q b (t h w)", t=4),
            )

        def load_x(b0, b1):
            nc.sync.dma_start(
                out=x_sb[:, b0:b1].rearrange("p b t w -> p b (t w)"),
                in_=x[b0:b1].rearrange("b (p t) h w -> p b (t h w)", t=4),
            )

        for tok in LOADS.split(" "):
            lo, hi = int(tok[1]), int(tok[2])
            {"w": lambda lo, hi: load_w(0, lo, hi), "d": lambda lo, hi: load_d(0, lo, hi), "x": load_x}[tok[0]](lo, hi)
        def load_class(k):
            load_w(k)
            load_d(k, 0, 2)
            load_d(k, 2, 4)

        for k in range(1, AHEAD):
            load_class(k)

        zeros_b = const.tile([P, NW], BF16)
        nc.vector.memset(zeros_b[:], 0.0)
        ident_f = const.tile([P, P], F32)
        make_identity(nc, ident_f[:])
        ident_b = const.tile([P, P], BF16)
        make_identity(nc, ident_b[:])
        ones_b = const.tile([P, 1], BF16)
        nc.vector.memset(ones_b[:], 1.0)
        warm = const.tile([P, 1], F32)
        nc.vector.memset(warm[:], 0.0)
        warm2 = const.tile([P, 1], F32)
        nc.scalar.activation(out=warm2[:], in_=warm[:], func=ACT.Exp)
        ones_f = const.tile([P, P], F32)
        nc.vector.memset(ones_f[:], 1.0 / NW)
        pad = const.tile([P, P], F32)
        nc.vector.memset(pad[:], 0.0)

        def w_t(k, g):
            wf = state[("w_raw", k)][:].bitcast(F32)
            wt = psum.tile([P, 4, P], F32, name="wt%d_%d" % (k, g), tag="bank")
            for tt in range(2):
                for u in range(2):
                    nc.tensor.transpose(wt[:, tt * 2 + u, :], wf[:, 2 * g + tt, u : 2 * P : 2], ident_f[:])
            state[("wt", k, g)] = wt

        def w_exit(k, g, eng="s"):
            if ("wg", k) not in state:
                wg_new = grp.tile([P, NC, 4], BF16, name="wg%d" % k, tag="wg", align_bytes=64)
                state[("wg", k)] = wg_new
            wgf = state[("wg", k)][:].bitcast(F32)
            o = wgf[:, g * 256 : (g + 1) * 256, :].rearrange("q (tt p) u -> q tt p u", tt=2)
            i = state[("wt", k, g)][:].rearrange("q (tt u) p -> q tt p u", u=2)
            if eng == "s":
                nc.scalar.copy(out=o, in_=i)
            else:
                nc.vector.tensor_copy(out=o, in_=i)

        def q_w(k):
            wg = state[("wg", k)]
            wc = mx.tile([P, NC], U32, name="wc%d" % k, tag="wc", align_bytes=64)
            ws = mx.tile([P, NC], U8, name="ws%d" % k, tag="ws", align_bytes=64)
            nc.vector.quantize_mx(out=wc[:].bitcast(FP8X4), scales=ws[:], in_=wg[:].rearrange("q c t -> q (c t)"))
            state[("wc", k)] = wc
            state[("ws", k)] = ws

        def dg_of(k, b):
            key = ("dg", k, b // 2)
            if key not in state:
                dg_new = grp.tile([P, 2, NW, 4], BF16, name="dg%d_%d" % (k, b // 2), tag="dg%d" % (b // 2), align_bytes=64, bufs=GRP if b < 2 else GRP1)
                state[key] = dg_new
            return state[key]

        def rg(k, b, n, h0, h1, eng):
            if eng == "G":
                ws = slice(h0 * NW // 2, h1 * NW // 2)
                nc.gpsimd.tensor_scalar(
                    out=dg_of(k, b)[:, b % 2, ws],
                    in0=state[("d_raw", k)][:, b, :, ws].rearrange("q t w -> q w t"),
                    scalar1=1.0,
                    scalar2=0.0,
                    op0=ALU.mult,
                    op1=ALU.add,
                )
                return
            cs = slice(h0 * 32, h1 * 32)
            if n == 2:
                src = state[("d_raw", k)][:, b : b + 2].rearrange("q b t (c i) -> q b c t i", i=4)
                dst = dg_of(k, b)[:].rearrange("q b (c i) t -> q b c t i", i=4)
            else:
                src = state[("d_raw", k)][:, b].rearrange("q t (c i) -> q c t i", i=4)[:, cs]
                dst = dg_of(k, b)[:, b % 2].rearrange("q (c i) t -> q c t i", i=4)[:, cs]
            if eng == "V":
                nc.vector.tensor_copy(out=dst, in_=src)
            else:
                nc.scalar.copy(out=dst, in_=src)

        def q_d_cols(k, b0, b1):
            if ("dc", k) not in state:
                dc_new = mx.tile([P, NB * NW], U32, name="dc%d" % k, tag="dc", align_bytes=64)
                ds_new = mx.tile([P, NB * NW], U8, name="ds%d" % k, tag="ds", align_bytes=64)
                state[("dc", k)] = dc_new
                state[("ds", k)] = ds_new
            cols = slice(b0 * NW, b1 * NW)
            nc.vector.quantize_mx(
                out=state[("dc", k)][:, cols].bitcast(FP8X4),
                scales=state[("ds", k)][:, cols],
                in_=dg_of(k, b0)[:, b0 % 2 : b0 % 2 + b1 - b0].rearrange("q b w t -> q (b w t)"),
            )

        def q_d(k, bp):
            q_d_cols(k, 2 * bp, 2 * bp + 2)

        def warm_up():
            if "warm" not in state:
                state["warm"] = psum.tile([P, NW], F32, name="warm_out", tag="bank")
            nc.tensor.matmul(out=state["warm"][:], lhsT=zeros_b[:, 0:P], rhs=zeros_b[:], start=True, stop=True)

        def x_tr(b):
            xp = psum.tile([P, 2, NC], BF16, name="xp%d" % b, tag="bank")
            for h in range(2):
                for t in range(4):
                    nc.tensor.transpose(xp[:, h, t * P : (t + 1) * P], x_sb[:, b, t, h * P : (h + 1) * P], ident_b[:])
            state[("xp", b)] = xp

        def x_exit(b):
            nc.scalar.copy(out=x_t[:, 2 * b : 2 * b + 2, :], in_=state[("xp", b)][:])

        def x_sum(b):
            if b == 0:
                state["sxp"] = psum.tile([P, 8], F32, name="sxp", tag="bank")
            for h in range(2):
                for t in range(4):
                    nc.tensor.matmul(
                        out=state["sxp"][:, 2 * b + h : 2 * b + h + 1],
                        lhsT=x_sb[:, b, t, h * P : (h + 1) * P],
                        rhs=ones_b[:],
                        start=(t == 0),
                        stop=(t == 3),
                    )

        def x_scale():
            nc.vector.tensor_copy(out=sx[:], in_=state["sxp"][:])
            for i in ABS:
                c0 = col_of(0, i)
                nc.vector.tensor_scalar_mul(
                    out=sr[:, c0 : c0 + 2 * (NK - 1) : 2],
                    in0=sx[:, i : i + 1].to_broadcast([P, NK - 1]),
                    scalar1=-1.0,
                )

        def direct(k, i):
            return i in ABS and k < NK - 1

        def ops(k):
            return state[("wc", k)], state[("ws", k)], state[("dc", k)], state[("ds", k)]

        def mm_a(k, i):
            bp, t = divmod(i, 4)
            wc, ws, dc, ds = ops(k)
            pa = psum.tile([P, 512], F32, name="pa%d_%d" % (k, i), tag="bank")
            mc = slice(t * P, (t + 1) * P)
            ncol = slice(bp * 512, (bp + 1) * 512)
            nc.tensor.matmul_mx(
                out=pa[:],
                lhsT=wc[:, mc].bitcast(FP8X4),
                lhsT_scale=ws[:, mc],
                rhs=dc[:, ncol].bitcast(FP8X4),
                rhs_scale=ds[:, ncol],
                start=True,
                stop=True,
            )
            state[("pa", k, i)] = pa

        def copy_a(k, i, eng):
            bp, t = divmod(i, 4)
            n = FINE[k][bp]
            key = ("rec", k, bp, t // n)
            if key not in state:
                rec_new = recp.tile([P, 2, n, NW], F32, name="rec%d_%d_%d" % (k, bp, t // n), tag="rec")
                state[key] = [rec_new, 0]
            rec = state[key][0]
            o = rec[:, :, t % n, :]
            s = state[("pa", k, i)][:].rearrange("p (b w) -> p b w", b=2)
            if eng == "s":
                nc.scalar.copy(out=o, in_=s)
            else:
                nc.vector.tensor_copy(out=o, in_=s)
            state[key][1] += 1
            if state[key][1] == n:
                t0 = t // n * n
                nc.sync.dma_start(
                    out=out_2[2 * bp : 2 * bp + 2, k].rearrange("b (p t) h w -> p b t (h w)", t=4)[:, :, t0 : t0 + n],
                    in_=rec[:],
                )
                if bp == 0 and t0 == 0 and k + AHEAD < NK:
                    load_class(k + AHEAD)

        def mm_b(k, i):
            wc, ws, dc, ds = ops(k)
            mc = slice(i * P, (i + 1) * P)
            pb = psum.tile([P, 512], F32, name="pb%d_%d" % (k, i), tag="bank")
            nc.tensor.matmul_mx(
                out=pb[:],
                lhsT=dc[:, mc].bitcast(FP8X4),
                lhsT_scale=ds[:, mc],
                rhs=wc[:].bitcast(FP8X4),
                rhs_scale=ws[:],
                start=True,
                stop=True,
            )
            state[("pb", k, i)] = pb

        def mm_c(k, i):
            wc, ws, dc, ds = ops(k)
            mc = slice(i * P, (i + 1) * P)
            if ("pc", k, i // 4) not in state:
                pc_new = psum.tile([P, 4, P], F32, name="pc%d_%d" % (k, i), tag="bank")
                state[("pc", k, i // 4)] = pc_new
            pc = state[("pc", k, i // 4)]
            for t in range(4):
                tcol = slice(t * P, (t + 1) * P)
                nc.tensor.matmul_mx(
                    out=pc[:, i % 4, :],
                    lhsT=dc[:, mc].bitcast(FP8X4),
                    lhsT_scale=ds[:, mc],
                    rhs=wc[:, tcol].bitcast(FP8X4),
                    rhs_scale=ws[:, tcol],
                    start=(t == 0),
                    stop=(t == 3),
                )

        def col_of(k, i):
            return (i // 2) * 16 + k * 2 + (i % 2)

        def stt(k, i):
            col = col_of(k, i)
            jk = junk.tile([P, 512], BF16, name="jk%d_%d" % (k, i), tag="jk")
            nc.vector.scalar_tensor_tensor(
                out=jk[:],
                in0=state[("pb", k, i)][:],
                scalar=1.0,
                in1=x_t[:, i, :],
                op0=ALU.mult,
                op1=ALU.max,
                accum_out=smax[:, col : col + 1],
            )

        def diff(k, i):
            df = junk.tile([P, 512], F32, name="df%d_%d" % (k, i), tag="df")
            nc.vector.tensor_tensor(out=df[:], in0=state[("pb", k, i)][:], in1=x_t[:, i, :], op=ALU.subtract)
            state[("df", k, i)] = df

        def absacc(k, i):
            col = col_of(k, i)
            ja = junk.tile([P, 512], BF16, name="ja%d_%d" % (k, i), tag="ja")
            nc.scalar.activation(
                out=ja[:], in_=state[("df", k, i)][:], func=ACT.Abs, scale=0.5, accum_out=smax[:, col : col + 1]
            )

        def creduce(k, g):
            dst = sr[:, g * 32 : g * 32 + 32].rearrange("p (b k h) -> p b k h", b=2, k=NK)[:, :, k, :]
            nc.vector.tensor_reduce(
                out=dst, in_=state[("pc", k, g)][:].rearrange("p (b h) c -> p b h c", b=2), axis=AX.X, op=ALU.add
            )

        def cacc(k, i):
            col = col_of(k, i)
            jc = junk.tile([P, P], BF16, name="jc%d_%d" % (k, i), tag="jc")
            nc.scalar.activation(
                out=jc[:], in_=state[("pc", k, i // 4)][:, i % 4, :], func=ACT.Copy, accum_out=sr[:, col : col + 1]
            )

        def v4(ap):
            return ap.rearrange("p (b k h) -> p b k h", k=NK, h=2)

        def bc(ap):
            return ap.rearrange("p (b h) -> p b h", h=2).unsqueeze(2).to_broadcast([P, ap.shape[1] // 2, NK, 2])

        def by_group(ap):
            return ap.rearrange("p (b k h) -> p b h k", k=NK, h=2)

        def groups(ap):
            return ap.rearrange("p (b h) -> p b h", h=2)

        srx = const.tile([P, 64], F32)

        def sum_rx():
            nc.vector.tensor_tensor(out=v4(srx[:]), in0=v4(sr[:]), in1=bc(sx[:]), op=ALU.add)

        def program(first, steady, odd, last):
            ops = []
            for k in range(NK):
                for tok in (first if k == 0 else last if k == NK - 1 else odd if k % 2 and odd else steady).split(" "):
                    if tok == "":
                        continue
                    kk = k + (1 if "+" in tok else 0)
                    if kk < NK:
                        ops.append((tok.replace("+", ""), kk))
            return ops

        progs = {
            "PE": program(PE_FIRST, PE_STEADY, PE_ODD, PE_LAST),
            "V": program(V_FIRST, V_STEADY, V_ODD, V_LAST),
            "S": program(S_FIRST, S_STEADY, S_ODD, S_LAST),
            "G": program(G_FIRST, G_STEADY, G_ODD, G_LAST),
        }
        order = {}
        done = set()
        live = [0]

        def imgs_ready(k, b):
            return (("r%d" % b, k) in done) or (("r%da" % b, k) in done and ("r%db" % b, k) in done)

        def quantised(k, i):
            if ("W", k) not in done:
                return False
            if k == 0 and i < 4:
                return ("d%d" % (i // 2), k) in done
            return ("D%d" % (i // 4), k) in done

        def ready(eng, op):
            t, k = op
            c = t[0]
            if (c in "TXba" or t in ("Y0", "c0", "c4")) and live[0] == BANKS:
                return False
            if c in "TX":
                return True
            if c in "YK":
                return True
            if c in "bc":
                return quantised(k, int(t[1]))
            if c == "a":
                i = int(t[1])
                return ("W", k) in done and (
                    (("d0", k) in done and ("d1", k) in done) if k == 0 and i < 4 else ("D%d" % (i // 4), k) in done
                )
            if t == "R":
                return all([("C%d" % j, NK - 1) in done or ("M%d" % (j // 4), NK - 1) in done for j in range(8)]) and ("xs", 0) in done
            if t == "xs":
                return ("Y3", 0) in done
            if c == "s":
                return ("b" + t[1], k) in done and ("x%d" % (int(t[1]) // 2), 0) in done
            if c == "M":
                return all([("c%d" % (4 * int(t[1]) + j), k) in done for j in range(4)])
            if c == "C":
                return all([("c%d" % j, k) in done for j in range(int(t[1]) // 4 * 4, int(t[1]) // 4 * 4 + 4) if not direct(k, j)])
            if c == "Z":
                return ("s" + t[1], k) in done
            if c == "A":
                return ("a" + t[1], k) in done
            if c == "e":
                return ("T" + t[1], k) in done
            if c == "x":
                return ("X" + t[1], k) in done
            if c == "W":
                return ("e0", k) in done and ("e1", k) in done
            if c == "D":
                return imgs_ready(k, 2 * int(t[1])) and imgs_ready(k, 2 * int(t[1]) + 1)
            if c == "d":
                return imgs_ready(k, int(t[1]))
            if c == "r":
                p = int(t[1]) // 2
                g = GRP if p == 0 else GRP1
                return k < g or ("D%d" % p, k - g) in done or (k == g and p == 0 and ("d1", 0) in done)
            return True

        def emit(eng, op):
            t, k = op
            c = t[0]
            n = 0 if t in ("W", "xs", "R") else int(t[1])
            if c == "T":
                w_t(k, n)
            elif c == "X":
                x_tr(n)
            elif c == "K":
                warm_up()
            elif c == "Y":
                x_sum(n)
            elif c == "b":
                mm_b(k, n)
            elif c == "c":
                mm_c(k, n)
            elif c == "a":
                mm_a(k, n)
            elif t == "xs":
                x_scale()
            elif t == "R":
                sum_rx()
            elif c == "s":
                if direct(k, n):
                    diff(k, n)
                else:
                    stt(k, n)
            elif c == "Z":
                absacc(k, n)
            elif c == "M":
                creduce(k, n)
            elif c == "C":
                cacc(k, n)
            elif c == "A":
                copy_a(k, n, "s" if eng == "S" else "v")
            elif c == "e":
                w_exit(k, n, "s" if eng == "S" else "v")
            elif c == "x":
                x_exit(n)
            elif c == "W":
                q_w(k)
            elif c == "D":
                q_d(k, n)
            elif c == "d":
                q_d_cols(k, n, n + 1)
            elif c == "r":
                half = {"a": (0, 1), "b": (1, 2)}.get(t[2:3], (0, 2))
                rg(k, n, 2 if t[2:3] == "p" else 1, half[0], half[1], eng)
                if t[2:3] == "p":
                    done.add(("r%d" % n, k))
                    done.add(("r%d" % (n + 1), k))
            if c in "TXba" or t in ("Y0", "c0", "c4"):
                live[0] += 1
            elif c in "esA" or t in ("C0", "C4", "xs", "M0", "M1") or (c == "x" and t != "xs"):
                live[0] -= 1
            done.add((t, k))

        left = {e: list(p) for e, p in progs.items()}
        while any(left.values()):
            moved = False
            for e in ("PE", "V", "S", "G"):
                while left[e] and ready(e, left[e][0]):
                    emit(e, left[e][0])
                    left[e] = left[e][1:]
                    moved = True
            assert moved, str({e: p[:2] for e, p in left.items()})

        halves = [(slice(0, 32), slice(0, 4)), (slice(32, 64), slice(4, 8))]
        t1 = const.tile([P, 64], F32)
        lg = const.tile([P, 64], F32)
        mxk = const.tile([P, 8], F32)
        sh = const.tile([P, 64], F32)
        ex = const.tile([P, 64], F32)
        den = const.tile([P, 8], F32)
        rden = const.tile([P, 8], F32)
        lsum = const.tile([P, 32], F32)
        for c, g in halves:
            nc.vector.scalar_tensor_tensor(
                out=t1[:, c], in0=smax[:, c], scalar=-2.0, in1=srx[:, c], op0=ALU.mult, op1=ALU.add
            )
        for c, g in halves:
            nc.vector.tensor_scalar(out=lg[:, c], in0=t1[:, c], scalar1=-5000.0, scalar2=5000.0, op0=ALU.max, op1=ALU.min)
        for c, g in halves:
            nc.vector.tensor_reduce(out=groups(mxk[:, g]), in_=by_group(lg[:, c]), axis=AX.X, op=ALU.max)
        for c, g in halves:
            nc.vector.tensor_tensor(out=v4(sh[:, c]), in0=v4(lg[:, c]), in1=bc(mxk[:, g]), op=ALU.subtract)
        for c, g in halves:
            nc.scalar.activation(out=ex[:, c], in_=sh[:, c], func=ACT.Exp, scale=0.1)
        for tok in S_TAIL.split(" "):
            if tok:
                emit("S", (tok, NK - 1))
        lg3 = lg[:].rearrange("p (c h) -> p c h", h=2)
        nc.vector.tensor_tensor(out=lsum[:], in0=lg3[:, :, 0], in1=lg3[:, :, 1], op=ALU.add)
        for tok in V_TAIL.split(" "):
            if tok:
                emit("V", (tok, NK - 1))
        pmean = psum.tile([P, 32], F32, name="pmean", tag="bank")
        nc.tensor.matmul(out=pmean[:], lhsT=ones_f[:], rhs=lsum[:], start=True, stop=True)
        for c, g in halves:
            nc.vector.tensor_reduce(out=groups(den[:, g]), in_=by_group(ex[:, c]), axis=AX.X, op=ALU.add)
        for c, g in halves:
            nc.vector.reciprocal(out=rden[:, g], in_=den[:, g])
        for c, g in halves:
            nc.vector.tensor_tensor(out=v4(pad[:, c]), in0=v4(ex[:, c]), in1=bc(rden[:, g]), op=ALU.mult)
        pt = psum.tile([P, P], F32, name="pt", tag="bank")
        nc.tensor.transpose(pt[:], pad[:], ident_f[:])
        e_sel = const.tile([P, NB, NK], F32)
        nc.vector.scalar_tensor_tensor(
            out=e_sel[:],
            in0=pmean[:].rearrange("p (b k) -> p b k", b=NB),
            scalar=0.1,
            in1=ident_f[:, 0:NB].unsqueeze(2).to_broadcast([P, NB, NK]),
            op0=ALU.mult,
            op1=ALU.mult,
        )
        e_out = const.tile([P, NK], F32)
        nc.vector.tensor_reduce(out=e_out[:], in_=e_sel[:].rearrange("p b k -> p k b"), axis=AX.X, op=ALU.add)
        nc.scalar.dma_start(out=out_1, in_=e_out[0:NB, :])
        p_out = const.tile([P, P], F32)
        nc.vector.tensor_copy(out=p_out[:], in_=pt[:])
        nc.scalar.dma_start(out=out_0.rearrange("b k (h r) w -> (b k h) (r w)", h=2), in_=p_out[0:64, :])
        for tok in S_TAIL2.split(" "):
            if tok:
                emit("S", (tok, NK - 1))
